import numpy as np
import ml_dtypes


def mxq(x, axis, fmt="e4m3"):
    dtype, down = {"e4m3": (ml_dtypes.float8_e4m3fn, 7), "e5m2": (ml_dtypes.float8_e5m2, 14)}[fmt]
    v = np.moveaxis(np.asarray(x, np.float32).astype(ml_dtypes.bfloat16).astype(np.float64), axis, -1)
    blocks = v.reshape(v.shape[:-1] + (-1, 32))
    amax = np.abs(blocks).max(-1, keepdims=True)
    byte = np.maximum(np.where(amax > 0, np.frexp(amax)[1] - 1 + 127, 0) - down, 1)
    scale = np.exp2(byte - 127.0)
    codes = (blocks / scale).astype(np.float32).astype(dtype).astype(np.float64)
    return np.moveaxis((codes * scale).reshape(v.shape), -1, axis)


WIDE = False


def mx_kscale(k):
    if not WIDE:
        return np.ones(k)
    levels = np.array([10, -10, 5, -5, 0])
    a = np.random.permutation(np.resize(levels, k // 512 * 4)).reshape(k // 512, 4)
    idx = np.arange(k)
    return np.exp2(a[idx // 512, idx % 128 // 32])


BF16 = ml_dtypes.bfloat16


def bf(x):
    return np.asarray(x, np.float32).astype(BF16)


def f64(x):
    return np.asarray(x).astype(np.float64)


M, DI, N, DO, TS = 8192, 1024, 512, 1024, 3
DENSITY = 0.25


def setup_inputs():
    k = mx_kscale(N)
    m = (np.random.uniform(size=(N, N)) < DENSITY).astype(np.float64)
    return {'state': bf(np.tanh(1.5 * np.random.standard_normal((M, N))) * k),
            'weights': bf(np.random.standard_normal((N, N)) * 1.5 / np.sqrt(DENSITY * N) / k[:, None]),
            'J': bf(np.random.standard_normal((N, N)) * 2.0 / np.sqrt(DENSITY * N)),
            'theta': bf(np.random.uniform(size=N) * 1.0 + 0.25),
            'lam': bf(0.35 + 0.05 * np.random.standard_normal(1)),
            'mask': bf(m * (1.0 - np.eye(N))),
            'noise_raw': bf(np.random.standard_normal((M, N)) * 2.5)}


def reference(state, weights, J, theta, lam, mask, noise_raw):
    st = f64(state)
    eff_w = f64(weights) * f64(mask)
    J_m = f64(J) * f64(mask)
    T = np.abs(np.sin(2.0 * f64(theta)))
    signal = mxq(st, 1, 'e4m3') @ mxq(eff_w, 0, 'e4m3')
    s = np.tanh(st)
    delta = (mxq(s, 1, 'e4m3') @ mxq(J_m, 0, 'e4m3')) * s
    noise = f64(noise_raw) * T * 0.1
    return np.tanh(signal + f64(lam) * delta + noise)

@@ -1,0 +1,222 @@
+from contextlib import ExitStack
+
+import concourse.mybir as mybir
+from concourse.masks import make_identity
+
+F32 = mybir.dt.float32
+BF16 = mybir.dt.bfloat16
+I32 = mybir.dt.int32
+U32 = mybir.dt.uint32
+U8 = mybir.dt.uint8
+FP8X4 = mybir.dt.float8_e4m3fn_x4
+ACT = mybir.ActivationFunctionType
+ALU = mybir.AluOpType
+
+P = 128
+ROWS = 8192
+NEUR = 512
+TPC = 4
+CHUNK = P * TPC
+N_CHUNKS = ROWS // CHUNK
+WIDE = TPC * NEUR
+
+FLOPS = 2 * 2 * ROWS * NEUR * NEUR
+
+PI_A = 3.140625
+PI_B = 9.67502593994140625e-4
+PI_C = 1.509957990978376e-7
+TWO_OVER_PI = 0.6366197723675814
+
+ACT_COPY_HALVES = (1,)
+
+
+def dve_add_tiles(c):
+    return 1 + (c % 2)
+
+
+def tile_brainquantumlayer_pb_t_kernel(tc, state, weights, J, theta, lam, mask, noise_raw, out):
+    nc = tc.nc
+    with ExitStack() as ctx:
+        const = ctx.enter_context(tc.tile_pool(name="const", bufs=1))
+        loads = ctx.enter_context(tc.tile_pool(name="loads", bufs=4))
+        packs = ctx.enter_context(tc.tile_pool(name="packs", bufs=3))
+        work = ctx.enter_context(tc.tile_pool(name="work", bufs=4))
+        ps_x = ctx.enter_context(tc.psum_pool(name="ps_x", bufs=2))
+        ps_s = ctx.enter_context(tc.psum_pool(name="ps_s", bufs=3))
+        ps_d = ctx.enter_context(tc.psum_pool(name="ps_d", bufs=3))
+
+        chunks = {}
+
+        def load(c):
+            rows = slice(c * CHUNK, (c + 1) * CHUNK)
+            st = loads.tile([P, WIDE], BF16, tag="st")
+            nc.sync.dma_start(
+                out=st[:].rearrange("p (j k) -> p j k", j=TPC),
+                in_=state[rows, :].rearrange("(p j) k -> p j k", j=TPC),
+            )
+            return st
+
+        def load_noise(c):
+            rows = slice(c * CHUNK, (c + 1) * CHUNK)
+            nz = loads.tile([P, WIDE], BF16, tag="nz")
+            nc.sync.dma_start(
+                out=nz[:].rearrange("p (j k) -> p j k", j=TPC),
+                in_=noise_raw[rows, :].rearrange("(p j) k -> p j k", j=TPC),
+            )
+            return nz
+
+        seed = const.tile([P, 1], F32)
+        nc.vector.memset(seed[:], 0.0)
+        seed_out = const.tile([P, 1], F32)
+        nc.scalar.activation(out=seed_out[:], in_=seed[:], func=ACT.Silu)
+
+        row0 = const.tile([P, NEUR + 32], BF16)
+        nc.vector.memset(row0[:], 0.0)
+        ones = const.tile([P, P], BF16)
+        nc.vector.memset(ones[:], 1.0)
+        nc.scalar.dma_start(out=row0[0:1, 0:NEUR], in_=theta.rearrange("(o n) -> o n", o=1))
+        nc.scalar.dma_start(out=row0[0:1, NEUR : NEUR + 1], in_=lam.rearrange("(o n) -> o n", o=1))
+        ident = const.tile([P, P], F32)
+        make_identity(nc, ident[:])
+
+        st0 = load(0)
+
+        def load_matrix(mat, nm):
+            raw = const.tile([P, 4, NEUR], BF16, name=nm)
+            nc.sync.dma_start(
+                out=raw[:].rearrange("p (u e) c -> p u e c", u=2),
+                in_=mat.rearrange("(u q e) c -> q u e c", u=2, e=2),
+            )
+            return raw
+
+        w_raw = load_matrix(weights, "w_raw")
+        m_raw = load_matrix(mask, "m_raw")
+        j_raw = load_matrix(J, "j_raw")
+        nz0 = load_noise(0)
+        chunks[0] = (st0, nz0)
+
+        thb = ps_s.tile([P, NEUR], F32, tag="sig")
+        nc.tensor.matmul(out=thb[:], lhsT=ones[:], rhs=row0[:, 0:NEUR], start=True, stop=True)
+        lmb = ps_d.tile([P, NEUR], F32, tag="dm")
+        nc.tensor.matmul(out=lmb[:, 0:32], lhsT=ones[:], rhs=row0[:, NEUR : NEUR + 32], start=True, stop=True)
+        lam_sb = const.tile([P, 1], F32)
+        nc.vector.tensor_copy(out=lam_sb[:], in_=lmb[:, 0:1])
+
+        k_int = const.tile([P, NEUR], I32)
+        nc.vector.tensor_scalar_mul(out=k_int[:], in0=thb[:], scalar1=TWO_OVER_PI)
+        ang = const.tile([P, NEUR], F32)
+        nc.vector.tensor_scalar_mul(out=ang[:], in0=thb[:], scalar1=2.0)
+        k_f = const.tile([P, NEUR], F32)
+        nc.vector.tensor_copy(out=k_f[:], in_=k_int[:])
+        for part in (PI_A, PI_B, PI_C):
+            nc.vector.scalar_tensor_tensor(
+                out=ang[:], in0=k_f[:], scalar=-part, in1=ang[:], op0=ALU.mult, op1=ALU.add
+            )
+        sin_t = const.tile([P, NEUR], F32)
+        nc.scalar.activation(out=sin_t[:], in_=ang[:], func=ACT.Sin)
+        t01 = const.tile([P, NEUR], F32)
+        nc.scalar.activation(out=t01[:], in_=sin_t[:], func=ACT.Abs, scale=0.1)
+
+        def prepare(raw, nm):
+            grouped = const.tile([P, 4 * NEUR], BF16, name=nm + "_g", align_bytes=64)
+            nc.vector.tensor_tensor(
+                out=grouped[:].rearrange("p (c t) -> p c t", t=4),
+                in0=raw[:].rearrange("p t c -> p c t"),
+                in1=m_raw[:].rearrange("p t c -> p c t"),
+                op=ALU.mult,
+            )
+            codes = const.tile([P, NEUR], U32, name=nm + "_c", align_bytes=64)
+            scales = const.tile([P, NEUR], U8, name=nm + "_s", align_bytes=64)
+            nc.vector.quantize_mx(out=codes[:].bitcast(FP8X4), scales=scales[:], in_=grouped[:])
+            return codes, scales
+
+        w_codes, w_scales = prepare(w_raw, "w")
+        j_codes, j_scales = prepare(j_raw, "j")
+
+        mids = {}
+
+        def front(c):
+            st, nz = chunks[c]
+            words = st[:].bitcast(F32)
+            gst = packs.tile([P, WIDE], BF16, tag="gst", align_bytes=64)
+            gw = gst[:].bitcast(F32).rearrange("p (r u) -> p r u", u=2)
+            for h in range(2):
+                xt = ps_x.tile([P, 2, 2 * P], F32, tag="xt")
+                for jj in range(2):
+                    j = 2 * h + jj
+                    for u in range(2):
+                        lo = 256 * j + P * u
+                        nc.tensor.transpose(xt[:, u, P * jj : P * jj + P], words[:, lo : lo + P], ident[:])
+                src = xt[:].rearrange("p u r -> p r u")
+                dst = gw[:, 256 * h : 256 * h + 256, :]
+                if h in ACT_COPY_HALVES:
+                    nc.scalar.copy(out=dst, in_=src)
+                else:
+                    nc.vector.tensor_copy(out=dst, in_=src)
+            s = work.tile([P, WIDE], F32, tag="s")
+            nc.scalar.activation(out=s[:], in_=st[:], func=ACT.Tanh)
+            gs = packs.tile([P, WIDE], BF16, tag="gs", align_bytes=64)
+            nc.scalar.activation(out=gs[:], in_=gst[:], func=ACT.Tanh)
+            nt = work.tile([P, WIDE], F32, tag="nt")
+            nc.gpsimd.tensor_tensor(
+                out=nt[:].rearrange("p (j n) -> p j n", j=TPC),
+                in0=nz[:].rearrange("p (j n) -> p j n", j=TPC),
+                in1=t01[:].unsqueeze(1).to_broadcast([P, TPC, NEUR]),
+                op=ALU.mult,
+            )
+            cst = packs.tile([P, NEUR], U32, tag="cst", align_bytes=64)
+            sst = packs.tile([P, NEUR], U8, tag="sst", align_bytes=64)
+            nc.vector.quantize_mx(out=cst[:].bitcast(FP8X4), scales=sst[:], in_=gst[:])
+            css = packs.tile([P, NEUR], U32, tag="css", align_bytes=64)
+            sss = packs.tile([P, NEUR], U8, tag="sss", align_bytes=64)
+            nc.vector.quantize_mx(out=css[:].bitcast(FP8X4), scales=sss[:], in_=gs[:])
+            mids[c] = (s, nt, cst, sst, css, sss)
+
+        def back(c):
+            s, nt, cst, sst, css, sss = mids[c]
+            for j in range(TPC):
+                m_cols = slice(P * j, P * j + P)
+                n_cols = slice(NEUR * j, NEUR * j + NEUR)
+                sig = ps_s.tile([P, NEUR], F32, tag="sig")
+                nc.tensor.matmul_mx(
+                    out=sig[:],
+                    lhsT=cst[:, m_cols].bitcast(FP8X4),
+                    lhsT_scale=sst[:, m_cols],
+                    rhs=w_codes[:].bitcast(FP8X4),
+                    rhs_scale=w_scales[:],
+                    start=True,
+                    stop=True,
+                )
+                dm = ps_d.tile([P, NEUR], F32, tag="dm")
+                nc.tensor.matmul_mx(
+                    out=dm[:],
+                    lhsT=css[:, m_cols].bitcast(FP8X4),
+                    lhsT_scale=sss[:, m_cols],
+                    rhs=j_codes[:].bitcast(FP8X4),
+                    rhs_scale=j_scales[:],
+                    start=True,
+                    stop=True,
+                )
+                nc.vector.tensor_tensor(out=nt[:, n_cols], in0=sig[:], in1=nt[:, n_cols], op=ALU.add)
+                nc.vector.scalar_tensor_tensor(
+                    out=s[:, n_cols], in0=dm[:], scalar=lam_sb[:, 0:1], in1=s[:, n_cols], op0=ALU.mult, op1=ALU.mult
+                )
+            split = NEUR * (TPC - dve_add_tiles(c))
+            nc.gpsimd.tensor_tensor(out=s[:, 0:split], in0=s[:, 0:split], in1=nt[:, 0:split], op=ALU.add)
+            nc.vector.tensor_tensor(out=s[:, split:WIDE], in0=s[:, split:WIDE], in1=nt[:, split:WIDE], op=ALU.add)
+            nc.scalar.activation(out=s[:], in_=s[:], func=ACT.Tanh)
+            rows = slice(c * CHUNK, (c + 1) * CHUNK)
+            nc.sync.dma_start(
+                out=out[rows, :].rearrange("(p j) n -> p j n", j=TPC),
+                in_=s[:].rearrange("p (j n) -> p j n", j=TPC),
+            )
+
+        for c in range(N_CHUNKS + 1):
+            if c + 1 < N_CHUNKS:
+                st_next = load(c + 1)
+                nz_next = load_noise(c + 1)
+                chunks[c + 1] = (st_next, nz_next)
+            if c < N_CHUNKS:
+                front(c)
+            if c >= 1:
+                back(c - 1)

@@ -27,11 +27,11 @@ PI_B = 9.67502593994140625e-4
 PI_C = 1.509957990978376e-7
 TWO_OVER_PI = 0.6366197723675814
 
-ACT_COPY_HALVES = (1,)
+ACT_COPY_HALVES = (0, 1)
 
 
 def dve_add_tiles(c):
-    return 1 + (c % 2)
+    return TPC
 
 
 def tile_brainquantumlayer_pb_t_kernel(tc, state, weights, J, theta, lam, mask, noise_raw, out):
@@ -74,8 +74,8 @@ def tile_brainquantumlayer_pb_t_kernel(tc, state, weights, J, theta, lam, mask, 
         nc.vector.memset(row0[:], 0.0)
         ones = const.tile([P, P], BF16)
         nc.vector.memset(ones[:], 1.0)
-        nc.scalar.dma_start(out=row0[0:1, 0:NEUR], in_=theta.rearrange("(o n) -> o n", o=1))
-        nc.scalar.dma_start(out=row0[0:1, NEUR : NEUR + 1], in_=lam.rearrange("(o n) -> o n", o=1))
+        nc.sync.dma_start(out=row0[0:1, 0:NEUR], in_=theta.rearrange("(o n) -> o n", o=1))
+        nc.sync.dma_start(out=row0[0:1, NEUR : NEUR + 1], in_=lam.rearrange("(o n) -> o n", o=1))
         ident = const.tile([P, P], F32)
         make_identity(nc, ident[:])
 
@@ -202,7 +202,8 @@ def tile_brainquantumlayer_pb_t_kernel(tc, state, weights, J, theta, lam, mask, 
                     out=s[:, n_cols], in0=dm[:], scalar=lam_sb[:, 0:1], in1=s[:, n_cols], op0=ALU.mult, op1=ALU.mult
                 )
             split = NEUR * (TPC - dve_add_tiles(c))
-            nc.gpsimd.tensor_tensor(out=s[:, 0:split], in0=s[:, 0:split], in1=nt[:, 0:split], op=ALU.add)
+            if split > 0:
+                nc.gpsimd.tensor_tensor(out=s[:, 0:split], in0=s[:, 0:split], in1=nt[:, 0:split], op=ALU.add)
             nc.vector.tensor_tensor(out=s[:, split:WIDE], in0=s[:, split:WIDE], in1=nt[:, split:WIDE], op=ALU.add)
             nc.scalar.activation(out=s[:], in_=s[:], func=ACT.Tanh)
             rows = slice(c * CHUNK, (c + 1) * CHUNK)

@@ -158,12 +158,9 @@ def tile_brainquantumlayer_pb_t_kernel(tc, state, weights, J, theta, lam, mask, 
             gs = packs.tile([P, WIDE], BF16, tag="gs", align_bytes=64)
             nc.scalar.activation(out=gs[:], in_=gst[:], func=ACT.Tanh)
             nt = work.tile([P, WIDE], F32, tag="nt")
-            nc.gpsimd.tensor_tensor(
-                out=nt[:].rearrange("p (j n) -> p j n", j=TPC),
-                in0=nz[:].rearrange("p (j n) -> p j n", j=TPC),
-                in1=t01[:].unsqueeze(1).to_broadcast([P, TPC, NEUR]),
-                op=ALU.mult,
-            )
+            for j in range(TPC):
+                n_cols = slice(NEUR * j, NEUR * j + NEUR)
+                nc.gpsimd.tensor_tensor(out=nt[:, n_cols], in0=nz[:, n_cols], in1=t01[:], op=ALU.mult)
             cst = packs.tile([P, NEUR], U32, tag="cst", align_bytes=64)
             sst = packs.tile([P, NEUR], U8, tag="sst", align_bytes=64)
             nc.vector.quantize_mx(out=cst[:].bitcast(FP8X4), scales=sst[:], in_=gst[:])

@@ -15,10 +15,11 @@ ALU = mybir.AluOpType
 P = 128
 ROWS = 8192
 NEUR = 512
-TPC = 4
-CHUNK = P * TPC
-N_CHUNKS = ROWS // CHUNK
-WIDE = TPC * NEUR
+TPG = 4
+GROUP = P * TPG
+NG = ROWS // GROUP
+WIDE = TPG * NEUR
+NB = 4
 
 FLOPS = 2 * 2 * ROWS * NEUR * NEUR
 
@@ -27,59 +28,70 @@ PI_B = 9.67502593994140625e-4
 PI_C = 1.509957990978376e-7
 TWO_OVER_PI = 0.6366197723675814
 
-ACT_COPY_HALVES = (0, 1)
-
-
-def dve_add_tiles(c):
-    return TPC
-
 
 def tile_brainquantumlayer_pb_t_kernel(tc, state, weights, J, theta, lam, mask, noise_raw, out):
     nc = tc.nc
     with ExitStack() as ctx:
         const = ctx.enter_context(tc.tile_pool(name="const", bufs=1))
-        loads = ctx.enter_context(tc.tile_pool(name="loads", bufs=4))
-        packs = ctx.enter_context(tc.tile_pool(name="packs", bufs=3))
-        work = ctx.enter_context(tc.tile_pool(name="work", bufs=4))
-        ps_x = ctx.enter_context(tc.psum_pool(name="ps_x", bufs=2))
-        ps_s = ctx.enter_context(tc.psum_pool(name="ps_s", bufs=3))
-        ps_d = ctx.enter_context(tc.psum_pool(name="ps_d", bufs=3))
+        loads = ctx.enter_context(tc.tile_pool(name="loads", bufs=3))
+        packs = ctx.enter_context(tc.tile_pool(name="packs", bufs=2))
+        work3 = ctx.enter_context(tc.tile_pool(name="work3", bufs=3))
+        work2 = ctx.enter_context(tc.tile_pool(name="work2", bufs=2))
+        ps_tp = ctx.enter_context(tc.psum_pool(name="ps_tp", bufs=2))
+        ps_nz = ctx.enter_context(tc.psum_pool(name="ps_nz", bufs=2))
+        ps_dm = ctx.enter_context(tc.psum_pool(name="ps_dm", bufs=2))
+        ps_sg = ctx.enter_context(tc.psum_pool(name="ps_sg", bufs=2))
+        ctx.enter_context(tc.manual_schedule())
 
-        chunks = {}
+        st_t = {}
+        nz_t = {}
+        gst_t = {}
+        gs_t = {}
+        sT_t = {}
+        nzt_t = {}
+        cst_t = {}
+        css_t = {}
+        dm_t = {}
+        sg_t = {}
+        cT_t = {}
+        o_t = {}
 
-        def load(c):
-            rows = slice(c * CHUNK, (c + 1) * CHUNK)
+        def ok(g):
+            return 0 <= g < NG
+
+        def ld(g):
+            if not ok(g):
+                return
+            rows = slice(g * GROUP, (g + 1) * GROUP)
             st = loads.tile([P, WIDE], BF16, tag="st")
             nc.sync.dma_start(
-                out=st[:].rearrange("p (j k) -> p j k", j=TPC),
-                in_=state[rows, :].rearrange("(p j) k -> p j k", j=TPC),
+                out=st[:].rearrange("p (j k) -> p j k", j=TPG),
+                in_=state[rows, :].rearrange("(p j) k -> p j k", j=TPG),
             )
-            return st
-
-        def load_noise(c):
-            rows = slice(c * CHUNK, (c + 1) * CHUNK)
             nz = loads.tile([P, WIDE], BF16, tag="nz")
             nc.sync.dma_start(
-                out=nz[:].rearrange("p (j k) -> p j k", j=TPC),
-                in_=noise_raw[rows, :].rearrange("(p j) k -> p j k", j=TPC),
+                out=nz[:].rearrange("p (j k) -> p j k", j=TPG),
+                in_=noise_raw[rows, :].rearrange("(p j) k -> p j k", j=TPG),
             )
-            return nz
+            st_t[g] = st
+            nz_t[g] = nz
 
         seed = const.tile([P, 1], F32)
         nc.vector.memset(seed[:], 0.0)
         seed_out = const.tile([P, 1], F32)
         nc.scalar.activation(out=seed_out[:], in_=seed[:], func=ACT.Silu)
-
-        row0 = const.tile([P, NEUR + 32], BF16)
-        nc.vector.memset(row0[:], 0.0)
-        ones = const.tile([P, P], BF16)
-        nc.vector.memset(ones[:], 1.0)
-        nc.sync.dma_start(out=row0[0:1, 0:NEUR], in_=theta.rearrange("(o n) -> o n", o=1))
-        nc.sync.dma_start(out=row0[0:1, NEUR : NEUR + 1], in_=lam.rearrange("(o n) -> o n", o=1))
         ident = const.tile([P, P], F32)
         make_identity(nc, ident[:])
 
-        st0 = load(0)
+        th_c = const.tile([P, NB], BF16)
+        nc.sync.dma_start(
+            out=th_c[:].rearrange("p (u e) -> p u e", u=2),
+            in_=theta.rearrange("(u q e) -> q u e", u=2, e=2),
+        )
+        lam_bf = const.tile([P, 1], BF16)
+        nc.sync.dma_start(out=lam_bf[:], in_=lam.partition_broadcast(P))
+
+        ld(0)
 
         def load_matrix(mat, nm):
             raw = const.tile([P, 4, NEUR], BF16, name=nm)
@@ -89,132 +101,228 @@ def tile_brainquantumlayer_pb_t_kernel(tc, state, weights, J, theta, lam, mask, 
             )
             return raw
 
-        w_raw = load_matrix(weights, "w_raw")
-        m_raw = load_matrix(mask, "m_raw")
         j_raw = load_matrix(J, "j_raw")
-        nz0 = load_noise(0)
-        chunks[0] = (st0, nz0)
+        m_raw = load_matrix(mask, "m_raw")
+        w_raw = load_matrix(weights, "w_raw")
+        ld(1)
+        ld(2)
 
-        thb = ps_s.tile([P, NEUR], F32, tag="sig")
-        nc.tensor.matmul(out=thb[:], lhsT=ones[:], rhs=row0[:, 0:NEUR], start=True, stop=True)
-        lmb = ps_d.tile([P, NEUR], F32, tag="dm")
-        nc.tensor.matmul(out=lmb[:, 0:32], lhsT=ones[:], rhs=row0[:, NEUR : NEUR + 32], start=True, stop=True)
         lam_sb = const.tile([P, 1], F32)
-        nc.vector.tensor_copy(out=lam_sb[:], in_=lmb[:, 0:1])
-
-        k_int = const.tile([P, NEUR], I32)
-        nc.vector.tensor_scalar_mul(out=k_int[:], in0=thb[:], scalar1=TWO_OVER_PI)
-        ang = const.tile([P, NEUR], F32)
-        nc.vector.tensor_scalar_mul(out=ang[:], in0=thb[:], scalar1=2.0)
-        k_f = const.tile([P, NEUR], F32)
+        nc.vector.tensor_copy(out=lam_sb[:], in_=lam_bf[:])
+        k_int = const.tile([P, NB], I32)
+        nc.vector.tensor_scalar_mul(out=k_int[:], in0=th_c[:], scalar1=TWO_OVER_PI)
+        ang = const.tile([P, NB], F32)
+        nc.vector.tensor_scalar_mul(out=ang[:], in0=th_c[:], scalar1=2.0)
+        k_f = const.tile([P, NB], F32)
         nc.vector.tensor_copy(out=k_f[:], in_=k_int[:])
         for part in (PI_A, PI_B, PI_C):
             nc.vector.scalar_tensor_tensor(
                 out=ang[:], in0=k_f[:], scalar=-part, in1=ang[:], op0=ALU.mult, op1=ALU.add
             )
-        sin_t = const.tile([P, NEUR], F32)
-        nc.scalar.activation(out=sin_t[:], in_=ang[:], func=ACT.Sin)
-        t01 = const.tile([P, NEUR], F32)
-        nc.scalar.activation(out=t01[:], in_=sin_t[:], func=ACT.Abs, scale=0.1)
+        sin_t = const.tile([P, NB], F32)
+        t01 = const.tile([P, NB], F32)
+
+        def sine():
+            nc.scalar.activation(out=sin_t[:], in_=ang[:], func=ACT.Sin)
+            nc.scalar.activation(out=t01[:], in_=sin_t[:], func=ACT.Abs, scale=0.1)
 
         def prepare(raw, nm):
             grouped = const.tile([P, 4 * NEUR], BF16, name=nm + "_g", align_bytes=64)
-            nc.vector.tensor_tensor(
-                out=grouped[:].rearrange("p (c t) -> p c t", t=4),
-                in0=raw[:].rearrange("p t c -> p c t"),
-                in1=m_raw[:].rearrange("p t c -> p c t"),
-                op=ALU.mult,
-            )
+            for u in range(2):
+                nc.vector.tensor_tensor(
+                    out=grouped[:, 1024 * u : 1024 * u + 1024].rearrange("p (e q t) -> p e q t", e=2, t=4),
+                    in0=raw[:, :, 256 * u : 256 * u + 256].rearrange("p t (q e) -> p e q t", e=2),
+                    in1=m_raw[:, :, 256 * u : 256 * u + 256].rearrange("p t (q e) -> p e q t", e=2),
+                    op=ALU.mult,
+                )
             codes = const.tile([P, NEUR], U32, name=nm + "_c", align_bytes=64)
             scales = const.tile([P, NEUR], U8, name=nm + "_s", align_bytes=64)
             nc.vector.quantize_mx(out=codes[:].bitcast(FP8X4), scales=scales[:], in_=grouped[:])
             return codes, scales
 
-        w_codes, w_scales = prepare(w_raw, "w")
-        j_codes, j_scales = prepare(j_raw, "j")
-
-        mids = {}
-
-        def front(c):
-            st, nz = chunks[c]
-            words = st[:].bitcast(F32)
-            gst = packs.tile([P, WIDE], BF16, tag="gst", align_bytes=64)
-            gw = gst[:].bitcast(F32).rearrange("p (r u) -> p r u", u=2)
-            for h in range(2):
-                xt = ps_x.tile([P, 2, 2 * P], F32, tag="xt")
-                for jj in range(2):
-                    j = 2 * h + jj
-                    for u in range(2):
-                        lo = 256 * j + P * u
-                        nc.tensor.transpose(xt[:, u, P * jj : P * jj + P], words[:, lo : lo + P], ident[:])
-                src = xt[:].rearrange("p u r -> p r u")
-                dst = gw[:, 256 * h : 256 * h + 256, :]
-                if h in ACT_COPY_HALVES:
-                    nc.scalar.copy(out=dst, in_=src)
-                else:
-                    nc.vector.tensor_copy(out=dst, in_=src)
-            s = work.tile([P, WIDE], F32, tag="s")
-            nc.scalar.activation(out=s[:], in_=st[:], func=ACT.Tanh)
-            gs = packs.tile([P, WIDE], BF16, tag="gs", align_bytes=64)
-            nc.scalar.activation(out=gs[:], in_=gst[:], func=ACT.Tanh)
-            nt = work.tile([P, WIDE], F32, tag="nt")
-            for j in range(TPC):
-                n_cols = slice(NEUR * j, NEUR * j + NEUR)
-                nc.gpsimd.tensor_tensor(out=nt[:, n_cols], in0=nz[:, n_cols], in1=t01[:], op=ALU.mult)
-            cst = packs.tile([P, NEUR], U32, tag="cst", align_bytes=64)
-            sst = packs.tile([P, NEUR], U8, tag="sst", align_bytes=64)
-            nc.vector.quantize_mx(out=cst[:].bitcast(FP8X4), scales=sst[:], in_=gst[:])
-            css = packs.tile([P, NEUR], U32, tag="css", align_bytes=64)
-            sss = packs.tile([P, NEUR], U8, tag="sss", align_bytes=64)
-            nc.vector.quantize_mx(out=css[:].bitcast(FP8X4), scales=sss[:], in_=gs[:])
-            mids[c] = (s, nt, cst, sst, css, sss)
-
-        def back(c):
-            s, nt, cst, sst, css, sss = mids[c]
-            for j in range(TPC):
-                m_cols = slice(P * j, P * j + P)
-                n_cols = slice(NEUR * j, NEUR * j + NEUR)
-                sig = ps_s.tile([P, NEUR], F32, tag="sig")
-                nc.tensor.matmul_mx(
-                    out=sig[:],
-                    lhsT=cst[:, m_cols].bitcast(FP8X4),
-                    lhsT_scale=sst[:, m_cols],
-                    rhs=w_codes[:].bitcast(FP8X4),
-                    rhs_scale=w_scales[:],
-                    start=True,
-                    stop=True,
+        def trs(g, h):
+            if not ok(g):
+                return
+            if h == 0:
+                gst = packs.tile([P, WIDE], BF16, tag="gst", align_bytes=64)
+                gs = packs.tile([P, WIDE], BF16, tag="gs", align_bytes=64)
+                sT = work3.tile([P, NB, GROUP], F32, tag="sT")
+                gst_t[g] = gst
+                gs_t[g] = gs
+                sT_t[g] = sT
+            gst = gst_t[g]
+            gs = gs_t[g]
+            sT = sT_t[g]
+            words = st_t[g][:].bitcast(F32)
+            xt = ps_tp.tile([P, 512], F32, tag="tp")
+            for jj in range(2):
+                for u in range(2):
+                    lo = 256 * (2 * h + jj) + P * u
+                    nc.tensor.transpose(
+                        xt[:, 256 * u + P * jj : 256 * u + P * jj + P], words[:, lo : lo + P], ident[:]
+                    )
+            r_lo = 256 * h
+            nc.scalar.activation(
+                out=sT[:, :, r_lo : r_lo + 256].rearrange("p (u e) r -> p u e r", u=2),
+                in_=xt[:].bitcast(BF16).rearrange("p (u r e) -> p u e r", u=2, e=2),
+                func=ACT.Tanh,
+            )
+            nc.scalar.copy(
+                out=gst[:].bitcast(F32).rearrange("p (r u) -> p r u", u=2)[:, r_lo : r_lo + 256, :],
+                in_=xt[:].rearrange("p (u r) -> p r u", u=2),
+            )
+            for piece in range(2):
+                r0 = r_lo + P * piece
+                nc.gpsimd.tensor_scalar(
+                    out=gs[:, 4 * r0 : 4 * r0 + 512].rearrange("p (r t) -> p r t", t=4),
+                    in0=sT[:, :, r0 : r0 + P].rearrange("p t r -> p r t"),
+                    scalar1=1.0,
+                    scalar2=0.0,
+                    op0=ALU.mult,
+                    op1=ALU.add,
                 )
-                dm = ps_d.tile([P, NEUR], F32, tag="dm")
-                nc.tensor.matmul_mx(
-                    out=dm[:],
-                    lhsT=css[:, m_cols].bitcast(FP8X4),
-                    lhsT_scale=sss[:, m_cols],
-                    rhs=j_codes[:].bitcast(FP8X4),
-                    rhs_scale=j_scales[:],
-                    start=True,
-                    stop=True,
-                )
-                nc.vector.tensor_tensor(out=nt[:, n_cols], in0=sig[:], in1=nt[:, n_cols], op=ALU.add)
-                nc.vector.scalar_tensor_tensor(
-                    out=s[:, n_cols], in0=dm[:], scalar=lam_sb[:, 0:1], in1=s[:, n_cols], op0=ALU.mult, op1=ALU.mult
-                )
-            split = NEUR * (TPC - dve_add_tiles(c))
-            if split > 0:
-                nc.gpsimd.tensor_tensor(out=s[:, 0:split], in0=s[:, 0:split], in1=nt[:, 0:split], op=ALU.add)
-            nc.vector.tensor_tensor(out=s[:, split:WIDE], in0=s[:, split:WIDE], in1=nt[:, split:WIDE], op=ALU.add)
-            nc.scalar.activation(out=s[:], in_=s[:], func=ACT.Tanh)
-            rows = slice(c * CHUNK, (c + 1) * CHUNK)
-            nc.sync.dma_start(
-                out=out[rows, :].rearrange("(p j) n -> p j n", j=TPC),
-                in_=s[:].rearrange("p (j n) -> p j n", j=TPC),
+
+        def trn(g, u):
+            if not ok(g):
+                return
+            words = nz_t[g][:].bitcast(F32)
+            nzt = ps_nz.tile([P, 512], F32, tag="nzt")
+            for j in range(TPG):
+                lo = 256 * j + P * u
+                nc.tensor.transpose(nzt[:, P * j : P * j + P], words[:, lo : lo + P], ident[:])
+            nzt_t[(g, u)] = nzt
+
+        def quant(g, src_t, dst_t, tg):
+            if not ok(g):
+                return
+            codes = packs.tile([P, GROUP], U32, tag="c" + tg, align_bytes=64)
+            scales = packs.tile([P, GROUP], U8, tag="s" + tg, align_bytes=64)
+            nc.vector.quantize_mx(out=codes[:].bitcast(FP8X4), scales=scales[:], in_=src_t[g][:])
+            dst_t[g] = (codes, scales)
+
+        def mx(g, b, pool, tg, wts, moving_t, dst_t):
+            if not ok(g):
+                return
+            codes, scales = moving_t[g]
+            acc = pool.tile([P, GROUP], F32, tag=tg)
+            cols = slice(P * b, P * b + P)
+            nc.tensor.matmul_mx(
+                out=acc[:],
+                lhsT=wts[0][:, cols].bitcast(FP8X4),
+                lhsT_scale=wts[1][:, cols],
+                rhs=codes[:].bitcast(FP8X4),
+                rhs_scale=scales[:],
+                start=True,
+                stop=True,
+            )
+            dst_t[(g, b)] = acc
+
+        def v1(g, b):
+            if b == 0:
+                cT = work2.tile([P, NB, GROUP], F32, tag="cT")
+                cT_t[g] = cT
+            nc.vector.scalar_tensor_tensor(
+                out=cT_t[g][:, b, :],
+                in0=dm_t[(g, b)][:],
+                scalar=lam_sb[:, 0:1],
+                in1=sT_t[g][:, b, :],
+                op0=ALU.mult,
+                op1=ALU.mult,
             )
 
-        for c in range(N_CHUNKS + 1):
-            if c + 1 < N_CHUNKS:
-                st_next = load(c + 1)
-                nz_next = load_noise(c + 1)
-                chunks[c + 1] = (st_next, nz_next)
-            if c < N_CHUNKS:
-                front(c)
-            if c >= 1:
-                back(c - 1)
+        def v3(g, b):
+            view = nzt_t[(g, b // 2)][:].bitcast(BF16).rearrange("p (r e) -> p e r", e=2)
+            nc.vector.scalar_tensor_tensor(
+                out=cT_t[g][:, b, :],
+                in0=view[:, b % 2, :],
+                scalar=t01[:, b : b + 1],
+                in1=cT_t[g][:, b, :],
+                op0=ALU.mult,
+                op1=ALU.add,
+            )
+
+        def v2(g, b):
+            nc.vector.tensor_tensor(out=cT_t[g][:, b, :], in0=sg_t[(g, b)][:], in1=cT_t[g][:, b, :], op=ALU.add)
+
+        def store(g, j_lo, j_hi):
+            rows = slice(g * GROUP, (g + 1) * GROUP)
+            nc.sync.dma_start(
+                out=out[rows, :].rearrange("(p j) n -> p j n", j=TPG)[:, j_lo:j_hi, :],
+                in_=o_t[g][:, j_lo:j_hi, :],
+            )
+
+        def bk(g, j):
+            if not ok(g):
+                return
+            if j == 0:
+                o = work2.tile([P, TPG, NEUR], F32, tag="o")
+                o_t[g] = o
+            cb = ps_tp.tile([P, 512], F32, tag="tp")
+            for b in range(NB):
+                nc.tensor.transpose(cb[:, P * b : P * b + P], cT_t[g][:, b, P * j : P * j + P], ident[:])
+            nc.scalar.activation(
+                out=o_t[g][:, j, :].rearrange("p (u q e) -> p u q e", u=2, e=2),
+                in_=cb[:].rearrange("p (u e q) -> p u q e", u=2, e=2),
+                func=ACT.Tanh,
+            )
+            if g == NG - 1 and j == 1:
+                store(g, 0, 2)
+            if j == TPG - 1:
+                if g == NG - 1:
+                    store(g, 2, 4)
+                else:
+                    store(g, 0, 4)
+
+        trs(0, 0)
+        trs(0, 1)
+        sine()
+        j_w = prepare(j_raw, "j")
+        quant(0, gs_t, css_t, "ss")
+        w_w = prepare(w_raw, "w")
+        quant(0, gst_t, cst_t, "st")
+        trn(0, 0)
+        trn(0, 1)
+        trs(1, 0)
+        trs(1, 1)
+        mx(0, 0, ps_dm, "dm", j_w, css_t, dm_t)
+        mx(0, 1, ps_dm, "dm", j_w, css_t, dm_t)
+
+        for g in range(NG + 1):
+            live = ok(g)
+            ld(g + 3)
+            mx(g, 0, ps_sg, "sg", w_w, cst_t, sg_t)
+            mx(g, 1, ps_sg, "sg", w_w, cst_t, sg_t)
+            if live:
+                v1(g, 0)
+                v1(g, 1)
+            bk(g - 1, 0)
+            mx(g, 2, ps_dm, "dm", j_w, css_t, dm_t)
+            mx(g, 3, ps_dm, "dm", j_w, css_t, dm_t)
+            if live:
+                v3(g, 0)
+                v3(g, 1)
+            trs(g + 2, 0)
+            bk(g - 1, 1)
+            trn(g + 1, 0)
+            if live:
+                v2(g, 0)
+                v2(g, 1)
+            quant(g + 1, gs_t, css_t, "ss")
+            mx(g, 2, ps_sg, "sg", w_w, cst_t, sg_t)
+            mx(g, 3, ps_sg, "sg", w_w, cst_t, sg_t)
+            if live:
+                v1(g, 2)
+                v1(g, 3)
+            bk(g - 1, 2)
+            trs(g + 2, 1)
+            bk(g - 1, 3)
+            mx(g + 1, 0, ps_dm, "dm", j_w, css_t, dm_t)
+            mx(g + 1, 1, ps_dm, "dm", j_w, css_t, dm_t)
+            if live:
+                v3(g, 2)
+                v3(g, 3)
+            trn(g + 1, 1)
+            if live:
+                v2(g, 2)
+                v2(g, 3)
+            quant(g + 1, gst_t, cst_t, "st")

@@ -29,6 +29,9 @@ PI_C = 1.509957990978376e-7
 TWO_OVER_PI = 0.6366197723675814
 
 
+B_BLOCKS = (0, 1)
+
+
 def tile_brainquantumlayer_pb_t_kernel(tc, state, weights, J, theta, lam, mask, noise_raw, out):
     nc = tc.nc
     with ExitStack() as ctx:
@@ -37,44 +40,50 @@ def tile_brainquantumlayer_pb_t_kernel(tc, state, weights, J, theta, lam, mask, 
         packs = ctx.enter_context(tc.tile_pool(name="packs", bufs=2))
         work3 = ctx.enter_context(tc.tile_pool(name="work3", bufs=3))
         work2 = ctx.enter_context(tc.tile_pool(name="work2", bufs=2))
-        ps_tp = ctx.enter_context(tc.psum_pool(name="ps_tp", bufs=2))
-        ps_nz = ctx.enter_context(tc.psum_pool(name="ps_nz", bufs=2))
+        ps_tp = ctx.enter_context(tc.psum_pool(name="ps_tp", bufs=3))
+        ps_nz = ctx.enter_context(tc.psum_pool(name="ps_nz", bufs=1))
         ps_dm = ctx.enter_context(tc.psum_pool(name="ps_dm", bufs=2))
         ps_sg = ctx.enter_context(tc.psum_pool(name="ps_sg", bufs=2))
         ctx.enter_context(tc.manual_schedule())
 
         st_t = {}
         nz_t = {}
+        xt_t = {}
         gst_t = {}
         gs_t = {}
         sT_t = {}
         nzt_t = {}
+        nT_t = {}
         cst_t = {}
         css_t = {}
         dm_t = {}
         sg_t = {}
         cT_t = {}
+        cb_t = {}
         o_t = {}
 
         def ok(g):
             return 0 <= g < NG
 
-        def ld(g):
+        def by_scalar(g):
+            return 0 <= g < NG - 1
+
+        def load(g, src, dst_t, tg):
             if not ok(g):
                 return
             rows = slice(g * GROUP, (g + 1) * GROUP)
-            st = loads.tile([P, WIDE], BF16, tag="st")
+            t = loads.tile([P, WIDE], BF16, tag=tg)
             nc.sync.dma_start(
-                out=st[:].rearrange("p (j k) -> p j k", j=TPG),
-                in_=state[rows, :].rearrange("(p j) k -> p j k", j=TPG),
+                out=t[:].rearrange("p (j k) -> p j k", j=TPG),
+                in_=src[rows, :].rearrange("(p j) k -> p j k", j=TPG),
             )
-            nz = loads.tile([P, WIDE], BF16, tag="nz")
-            nc.sync.dma_start(
-                out=nz[:].rearrange("p (j k) -> p j k", j=TPG),
-                in_=noise_raw[rows, :].rearrange("(p j) k -> p j k", j=TPG),
-            )
-            st_t[g] = st
-            nz_t[g] = nz
+            dst_t[g] = t
+
+        def lds(g):
+            load(g, state, st_t, "st")
+
+        def ldn(g):
+            load(g, noise_raw, nz_t, "nz")
 
         seed = const.tile([P, 1], F32)
         nc.vector.memset(seed[:], 0.0)
@@ -91,7 +100,7 @@ def tile_brainquantumlayer_pb_t_kernel(tc, state, weights, J, theta, lam, mask, 
         lam_bf = const.tile([P, 1], BF16)
         nc.sync.dma_start(out=lam_bf[:], in_=lam.partition_broadcast(P))
 
-        ld(0)
+        lds(0)
 
         def load_matrix(mat, nm):
             raw = const.tile([P, 4, NEUR], BF16, name=nm)
@@ -104,8 +113,11 @@ def tile_brainquantumlayer_pb_t_kernel(tc, state, weights, J, theta, lam, mask, 
         j_raw = load_matrix(J, "j_raw")
         m_raw = load_matrix(mask, "m_raw")
         w_raw = load_matrix(weights, "w_raw")
-        ld(1)
-        ld(2)
+        ldn(0)
+        lds(1)
+        ldn(1)
+        lds(2)
+        ldn(2)
 
         lam_sb = const.tile([P, 1], F32)
         nc.vector.tensor_copy(out=lam_sb[:], in_=lam_bf[:])
@@ -140,7 +152,20 @@ def tile_brainquantumlayer_pb_t_kernel(tc, state, weights, J, theta, lam, mask, 
             nc.vector.quantize_mx(out=codes[:].bitcast(FP8X4), scales=scales[:], in_=grouped[:])
             return codes, scales
 
-        def trs(g, h):
+        def trs_pe(g, h):
+            if not ok(g):
+                return
+            words = st_t[g][:].bitcast(F32)
+            xt = ps_tp.tile([P, 512], F32, tag="tp")
+            for jj in range(2):
+                for u in range(2):
+                    lo = 256 * (2 * h + jj) + P * u
+                    nc.tensor.transpose(
+                        xt[:, 256 * u + P * jj : 256 * u + P * jj + P], words[:, lo : lo + P], ident[:]
+                    )
+            xt_t[(g, h)] = xt
+
+        def trs_out(g, h, round_on_scalar):
             if not ok(g):
                 return
             if h == 0:
@@ -153,34 +178,34 @@ def tile_brainquantumlayer_pb_t_kernel(tc, state, weights, J, theta, lam, mask, 
             gst = gst_t[g]
             gs = gs_t[g]
             sT = sT_t[g]
-            words = st_t[g][:].bitcast(F32)
-            xt = ps_tp.tile([P, 512], F32, tag="tp")
-            for jj in range(2):
-                for u in range(2):
-                    lo = 256 * (2 * h + jj) + P * u
-                    nc.tensor.transpose(
-                        xt[:, 256 * u + P * jj : 256 * u + P * jj + P], words[:, lo : lo + P], ident[:]
-                    )
+            xt = xt_t[(g, h)]
             r_lo = 256 * h
             nc.scalar.activation(
                 out=sT[:, :, r_lo : r_lo + 256].rearrange("p (u e) r -> p u e r", u=2),
                 in_=xt[:].bitcast(BF16).rearrange("p (u r e) -> p u e r", u=2, e=2),
                 func=ACT.Tanh,
             )
+            if round_on_scalar:
+                nc.scalar.activation(
+                    out=gs[:, 4 * r_lo : 4 * r_lo + 1024].rearrange("p (r u e) -> p r u e", u=2, e=2),
+                    in_=xt[:].bitcast(BF16).rearrange("p (u r e) -> p r u e", u=2, e=2),
+                    func=ACT.Tanh,
+                )
             nc.scalar.copy(
                 out=gst[:].bitcast(F32).rearrange("p (r u) -> p r u", u=2)[:, r_lo : r_lo + 256, :],
                 in_=xt[:].rearrange("p (u r) -> p r u", u=2),
             )
-            for piece in range(2):
-                r0 = r_lo + P * piece
-                nc.gpsimd.tensor_scalar(
-                    out=gs[:, 4 * r0 : 4 * r0 + 512].rearrange("p (r t) -> p r t", t=4),
-                    in0=sT[:, :, r0 : r0 + P].rearrange("p t r -> p r t"),
-                    scalar1=1.0,
-                    scalar2=0.0,
-                    op0=ALU.mult,
-                    op1=ALU.add,
-                )
+            if not round_on_scalar:
+                for piece in range(2):
+                    r0 = r_lo + P * piece
+                    nc.gpsimd.tensor_scalar(
+                        out=gs[:, 4 * r0 : 4 * r0 + 512].rearrange("p (r t) -> p r t", t=4),
+                        in0=sT[:, :, r0 : r0 + P].rearrange("p t r -> p r t"),
+                        scalar1=1.0,
+                        scalar2=0.0,
+                        op0=ALU.mult,
+                        op1=ALU.add,
+                    )
 
         def trn(g, u):
             if not ok(g):
@@ -192,6 +217,17 @@ def tile_brainquantumlayer_pb_t_kernel(tc, state, weights, J, theta, lam, mask, 
                 nc.tensor.transpose(nzt[:, P * j : P * j + P], words[:, lo : lo + P], ident[:])
             nzt_t[(g, u)] = nzt
 
+        def noise_view(g, b):
+            return nzt_t[(g, b // 2)][:].bitcast(BF16).rearrange("p (r e) -> p e r", e=2)[:, b % 2, :]
+
+        def n1(g, b):
+            if b == B_BLOCKS[0]:
+                nT = work2.tile([P, len(B_BLOCKS), GROUP], F32, tag="nT")
+                nT_t[g] = nT
+            nc.scalar.activation(
+                out=nT_t[g][:, B_BLOCKS.index(b), :], in_=noise_view(g, b), func=ACT.Copy, scale=t01[:, b : b + 1]
+            )
+
         def quant(g, src_t, dst_t, tg):
             if not ok(g):
                 return
@@ -199,6 +235,12 @@ def tile_brainquantumlayer_pb_t_kernel(tc, state, weights, J, theta, lam, mask, 
             scales = packs.tile([P, GROUP], U8, tag="s" + tg, align_bytes=64)
             nc.vector.quantize_mx(out=codes[:].bitcast(FP8X4), scales=scales[:], in_=src_t[g][:])
             dst_t[g] = (codes, scales)
+
+        def qs(g):
+            quant(g, gs_t, css_t, "ss")
+
+        def qt(g):
+            quant(g, gst_t, cst_t, "st")
 
         def mx(g, b, pool, tg, wts, moving_t, dst_t):
             if not ok(g):
@@ -218,8 +260,10 @@ def tile_brainquantumlayer_pb_t_kernel(tc, state, weights, J, theta, lam, mask, 
             dst_t[(g, b)] = acc
 
         def v1(g, b):
-            if b == 0:
-                cT = work2.tile([P, NB, GROUP], F32, tag="cT")
+            if not ok(g):
+                return
+            if g not in cT_t:
+                cT = work3.tile([P, NB, GROUP], F32, tag="cT")
                 cT_t[g] = cT
             nc.vector.scalar_tensor_tensor(
                 out=cT_t[g][:, b, :],
@@ -231,10 +275,11 @@ def tile_brainquantumlayer_pb_t_kernel(tc, state, weights, J, theta, lam, mask, 
             )
 
         def v3(g, b):
-            view = nzt_t[(g, b // 2)][:].bitcast(BF16).rearrange("p (r e) -> p e r", e=2)
+            if not ok(g):
+                return
             nc.vector.scalar_tensor_tensor(
                 out=cT_t[g][:, b, :],
-                in0=view[:, b % 2, :],
+                in0=noise_view(g, b),
                 scalar=t01[:, b : b + 1],
                 in1=cT_t[g][:, b, :],
                 op0=ALU.mult,
@@ -242,7 +287,14 @@ def tile_brainquantumlayer_pb_t_kernel(tc, state, weights, J, theta, lam, mask, 
             )
 
         def v2(g, b):
-            nc.vector.tensor_tensor(out=cT_t[g][:, b, :], in0=sg_t[(g, b)][:], in1=cT_t[g][:, b, :], op=ALU.add)
+            if not ok(g):
+                return
+            if by_scalar(g) and b in B_BLOCKS:
+                part = nT_t[g][:, B_BLOCKS.index(b), :]
+                nc.vector.tensor_tensor(out=part, in0=sg_t[(g, b)][:], in1=part, op=ALU.add)
+                nc.gpsimd.tensor_tensor(out=cT_t[g][:, b, :], in0=cT_t[g][:, b, :], in1=part, op=ALU.add)
+            else:
+                nc.vector.tensor_tensor(out=cT_t[g][:, b, :], in0=sg_t[(g, b)][:], in1=cT_t[g][:, b, :], op=ALU.add)
 
         def store(g, j_lo, j_hi):
             rows = slice(g * GROUP, (g + 1) * GROUP)
@@ -251,78 +303,100 @@ def tile_brainquantumlayer_pb_t_kernel(tc, state, weights, J, theta, lam, mask, 
                 in_=o_t[g][:, j_lo:j_hi, :],
             )
 
-        def bk(g, j):
+        def bk_pe(g, j):
+            if not ok(g):
+                return
+            cb = ps_tp.tile([P, 512], F32, tag="tp")
+            for b in range(NB):
+                nc.tensor.transpose(cb[:, P * b : P * b + P], cT_t[g][:, b, P * j : P * j + P], ident[:])
+            cb_t[(g, j)] = cb
+
+        def bk_out(g, j):
             if not ok(g):
                 return
             if j == 0:
                 o = work2.tile([P, TPG, NEUR], F32, tag="o")
                 o_t[g] = o
-            cb = ps_tp.tile([P, 512], F32, tag="tp")
-            for b in range(NB):
-                nc.tensor.transpose(cb[:, P * b : P * b + P], cT_t[g][:, b, P * j : P * j + P], ident[:])
             nc.scalar.activation(
                 out=o_t[g][:, j, :].rearrange("p (u q e) -> p u q e", u=2, e=2),
-                in_=cb[:].rearrange("p (u e q) -> p u q e", u=2, e=2),
+                in_=cb_t[(g, j)][:].rearrange("p (u e q) -> p u q e", u=2, e=2),
                 func=ACT.Tanh,
             )
-            if g == NG - 1 and j == 1:
-                store(g, 0, 2)
-            if j == TPG - 1:
-                if g == NG - 1:
-                    store(g, 2, 4)
-                else:
-                    store(g, 0, 4)
+            if g == NG - 1:
+                store(g, j, j + 1)
+            elif j == TPG - 1:
+                store(g, 0, TPG)
 
-        trs(0, 0)
-        trs(0, 1)
+        trs_pe(0, 0)
+        trs_pe(0, 1)
+        trs_out(0, 0, True)
+        trs_out(0, 1, True)
         sine()
         j_w = prepare(j_raw, "j")
-        quant(0, gs_t, css_t, "ss")
         w_w = prepare(w_raw, "w")
-        quant(0, gst_t, cst_t, "st")
-        trn(0, 0)
-        trn(0, 1)
-        trs(1, 0)
-        trs(1, 1)
-        mx(0, 0, ps_dm, "dm", j_w, css_t, dm_t)
-        mx(0, 1, ps_dm, "dm", j_w, css_t, dm_t)
 
-        for g in range(NG + 1):
-            live = ok(g)
-            ld(g + 3)
-            mx(g, 0, ps_sg, "sg", w_w, cst_t, sg_t)
-            mx(g, 1, ps_sg, "sg", w_w, cst_t, sg_t)
-            if live:
-                v1(g, 0)
-                v1(g, 1)
-            bk(g - 1, 0)
-            mx(g, 2, ps_dm, "dm", j_w, css_t, dm_t)
-            mx(g, 3, ps_dm, "dm", j_w, css_t, dm_t)
-            if live:
+        def dm(g, b):
+            mx(g, b, ps_dm, "dm", j_w, css_t, dm_t)
+
+        def sg(g, b):
+            mx(g, b, ps_sg, "sg", w_w, cst_t, sg_t)
+
+        qs(0)
+        qt(0)
+        trn(0, 0)
+        n1(0, 0)
+        n1(0, 1)
+        trs_pe(1, 0)
+        trs_out(1, 0, False)
+        trs_pe(1, 1)
+        trs_out(1, 1, False)
+        dm(0, 2)
+        dm(0, 3)
+        sg(0, 2)
+        sg(0, 3)
+
+        for g in range(NG + 2):
+            v1(g, 2)
+            v1(g, 3)
+            trn(g, 1)
+            lds(g + 3)
+            ldn(g + 3)
+            trs_pe(g + 2, 0)
+            bk_pe(g - 2, 3)
+            trs_pe(g + 2, 1)
+            trs_out(g + 2, 0, False)
+            bk_out(g - 2, 3)
+            v2(g, 2)
+            v2(g, 3)
+            dm(g, 0)
+            dm(g, 1)
+            sg(g, 0)
+            sg(g, 1)
+            trs_out(g + 2, 1, False)
+            v3(g, 2)
+            v3(g, 3)
+            if by_scalar(g + 1):
+                trn(g + 1, 0)
+                n1(g + 1, 0)
+                n1(g + 1, 1)
+            if g == NG - 1:
+                trn(g, 0)
+            qt(g + 1)
+            qs(g + 1)
+            bk_pe(g - 1, 0)
+            bk_pe(g - 1, 1)
+            bk_pe(g - 1, 2)
+            bk_out(g - 1, 0)
+            bk_out(g - 1, 1)
+            bk_out(g - 1, 2)
+            v1(g, 0)
+            v1(g, 1)
+            dm(g + 1, 2)
+            dm(g + 1, 3)
+            v2(g, 0)
+            v2(g, 1)
+            if g == NG - 1:
                 v3(g, 0)
                 v3(g, 1)
-            trs(g + 2, 0)
-            bk(g - 1, 1)
-            trn(g + 1, 0)
-            if live:
-                v2(g, 0)
-                v2(g, 1)
-            quant(g + 1, gs_t, css_t, "ss")
-            mx(g, 2, ps_sg, "sg", w_w, cst_t, sg_t)
-            mx(g, 3, ps_sg, "sg", w_w, cst_t, sg_t)
-            if live:
-                v1(g, 2)
-                v1(g, 3)
-            bk(g - 1, 2)
-            trs(g + 2, 1)
-            bk(g - 1, 3)
-            mx(g + 1, 0, ps_dm, "dm", j_w, css_t, dm_t)
-            mx(g + 1, 1, ps_dm, "dm", j_w, css_t, dm_t)
-            if live:
-                v3(g, 2)
-                v3(g, 3)
-            trn(g + 1, 1)
-            if live:
-                v2(g, 2)
-                v2(g, 3)
-            quant(g + 1, gst_t, cst_t, "st")
+            sg(g + 1, 2)
+            sg(g + 1, 3)

@@ -100,7 +100,16 @@ def tile_brainquantumlayer_pb_t_kernel(tc, state, weights, J, theta, lam, mask, 
         lam_bf = const.tile([P, 1], BF16)
         nc.sync.dma_start(out=lam_bf[:], in_=lam.partition_broadcast(P))
 
-        lds(0)
+        st_first = loads.tile([P, WIDE], BF16, tag="st")
+        st_t[0] = st_first
+
+        def first_half(h):
+            nc.sync.dma_start(
+                out=st_first[:, 1024 * h : 1024 * h + 1024].rearrange("p (j k) -> p j k", j=2),
+                in_=state[0:GROUP, :].rearrange("(p j) k -> p j k", j=TPG)[:, 2 * h : 2 * h + 2, :],
+            )
+
+        first_half(0)
 
         def load_matrix(mat, nm):
             raw = const.tile([P, 4, NEUR], BF16, name=nm)
@@ -112,6 +121,7 @@ def tile_brainquantumlayer_pb_t_kernel(tc, state, weights, J, theta, lam, mask, 
 
         j_raw = load_matrix(J, "j_raw")
         m_raw = load_matrix(mask, "m_raw")
+        first_half(1)
         w_raw = load_matrix(weights, "w_raw")
         ldn(0)
         lds(1)
@@ -196,16 +206,14 @@ def tile_brainquantumlayer_pb_t_kernel(tc, state, weights, J, theta, lam, mask, 
                 in_=xt[:].rearrange("p (u r) -> p r u", u=2),
             )
             if not round_on_scalar:
-                for piece in range(2):
-                    r0 = r_lo + P * piece
-                    nc.gpsimd.tensor_scalar(
-                        out=gs[:, 4 * r0 : 4 * r0 + 512].rearrange("p (r t) -> p r t", t=4),
-                        in0=sT[:, :, r0 : r0 + P].rearrange("p t r -> p r t"),
-                        scalar1=1.0,
-                        scalar2=0.0,
-                        op0=ALU.mult,
-                        op1=ALU.add,
-                    )
+                nc.gpsimd.tensor_scalar(
+                    out=gs[:, 4 * r_lo : 4 * r_lo + 1024].rearrange("p (r t) -> p r t", t=4),
+                    in0=sT[:, :, r_lo : r_lo + 256].rearrange("p t r -> p r t"),
+                    scalar1=1.0,
+                    scalar2=0.0,
+                    op0=ALU.mult,
+                    op1=ALU.add,
+                )
 
         def trn(g, u):
             if not ok(g):
@@ -292,7 +300,9 @@ def tile_brainquantumlayer_pb_t_kernel(tc, state, weights, J, theta, lam, mask, 
             if by_scalar(g) and b in B_BLOCKS:
                 part = nT_t[g][:, B_BLOCKS.index(b), :]
                 nc.vector.tensor_tensor(out=part, in0=sg_t[(g, b)][:], in1=part, op=ALU.add)
-                nc.gpsimd.tensor_tensor(out=cT_t[g][:, b, :], in0=cT_t[g][:, b, :], in1=part, op=ALU.add)
+                if b == B_BLOCKS[-1]:
+                    both = cT_t[g][:, B_BLOCKS[0] : B_BLOCKS[-1] + 1, :]
+                    nc.gpsimd.tensor_tensor(out=both, in0=both, in1=nT_t[g][:], op=ALU.add)
             else:
                 nc.vector.tensor_tensor(out=cT_t[g][:, b, :], in0=sg_t[(g, b)][:], in1=cT_t[g][:, b, :], op=ALU.add)
 
@@ -381,8 +391,6 @@ def tile_brainquantumlayer_pb_t_kernel(tc, state, weights, J, theta, lam, mask, 
                 n1(g + 1, 1)
             if g == NG - 1:
                 trn(g, 0)
-            qt(g + 1)
-            qs(g + 1)
             bk_pe(g - 1, 0)
             bk_pe(g - 1, 1)
             bk_pe(g - 1, 2)
@@ -391,6 +399,8 @@ def tile_brainquantumlayer_pb_t_kernel(tc, state, weights, J, theta, lam, mask, 
             bk_out(g - 1, 2)
             v1(g, 0)
             v1(g, 1)
+            qt(g + 1)
+            qs(g + 1)
             dm(g + 1, 2)
             dm(g + 1, 3)
             v2(g, 0)

@@ -65,9 +65,6 @@ def tile_brainquantumlayer_pb_t_kernel(tc, state, weights, J, theta, lam, mask, 
         def ok(g):
             return 0 <= g < NG
 
-        def by_scalar(g):
-            return 0 <= g < NG - 1
-
         def load(g, src, dst_t, tg):
             if not ok(g):
                 return
@@ -229,8 +226,10 @@ def tile_brainquantumlayer_pb_t_kernel(tc, state, weights, J, theta, lam, mask, 
             return nzt_t[(g, b // 2)][:].bitcast(BF16).rearrange("p (r e) -> p e r", e=2)[:, b % 2, :]
 
         def n1(g, b):
+            if not ok(g):
+                return
             if b == B_BLOCKS[0]:
-                nT = work2.tile([P, len(B_BLOCKS), GROUP], F32, tag="nT")
+                nT = work3.tile([P, len(B_BLOCKS), GROUP], F32, tag="nT")
                 nT_t[g] = nT
             nc.scalar.activation(
                 out=nT_t[g][:, B_BLOCKS.index(b), :], in_=noise_view(g, b), func=ACT.Copy, scale=t01[:, b : b + 1]
@@ -297,12 +296,9 @@ def tile_brainquantumlayer_pb_t_kernel(tc, state, weights, J, theta, lam, mask, 
         def v2(g, b):
             if not ok(g):
                 return
-            if by_scalar(g) and b in B_BLOCKS:
+            if b in B_BLOCKS:
                 part = nT_t[g][:, B_BLOCKS.index(b), :]
                 nc.vector.tensor_tensor(out=part, in0=sg_t[(g, b)][:], in1=part, op=ALU.add)
-                if b == B_BLOCKS[-1]:
-                    both = cT_t[g][:, B_BLOCKS[0] : B_BLOCKS[-1] + 1, :]
-                    nc.gpsimd.tensor_tensor(out=both, in0=both, in1=nT_t[g][:], op=ALU.add)
             else:
                 nc.vector.tensor_tensor(out=cT_t[g][:, b, :], in0=sg_t[(g, b)][:], in1=cT_t[g][:, b, :], op=ALU.add)
 
@@ -318,7 +314,21 @@ def tile_brainquantumlayer_pb_t_kernel(tc, state, weights, J, theta, lam, mask, 
                 return
             cb = ps_tp.tile([P, 512], F32, tag="tp")
             for b in range(NB):
-                nc.tensor.transpose(cb[:, P * b : P * b + P], cT_t[g][:, b, P * j : P * j + P], ident[:])
+                dst = cb[:, P * b : P * b + P]
+                if b in B_BLOCKS:
+                    nc.tensor.matmul(
+                        out=dst, lhsT=cT_t[g][:, b, P * j : P * j + P], rhs=ident[:], is_transpose=True, start=True, stop=False
+                    )
+                    nc.tensor.matmul(
+                        out=dst,
+                        lhsT=nT_t[g][:, B_BLOCKS.index(b), P * j : P * j + P],
+                        rhs=ident[:],
+                        is_transpose=True,
+                        start=False,
+                        stop=True,
+                    )
+                else:
+                    nc.tensor.transpose(dst, cT_t[g][:, b, P * j : P * j + P], ident[:])
             cb_t[(g, j)] = cb
 
         def bk_out(g, j):
@@ -332,10 +342,7 @@ def tile_brainquantumlayer_pb_t_kernel(tc, state, weights, J, theta, lam, mask, 
                 in_=cb_t[(g, j)][:].rearrange("p (u e q) -> p u q e", u=2, e=2),
                 func=ACT.Tanh,
             )
-            if g == NG - 1:
-                store(g, j, j + 1)
-            elif j == TPG - 1:
-                store(g, 0, TPG)
+            store(g, j, j + 1)
 
         trs_pe(0, 0)
         trs_pe(0, 1)
@@ -385,12 +392,9 @@ def tile_brainquantumlayer_pb_t_kernel(tc, state, weights, J, theta, lam, mask, 
             trs_out(g + 2, 1, False)
             v3(g, 2)
             v3(g, 3)
-            if by_scalar(g + 1):
-                trn(g + 1, 0)
-                n1(g + 1, 0)
-                n1(g + 1, 1)
-            if g == NG - 1:
-                trn(g, 0)
+            trn(g + 1, 0)
+            n1(g + 1, 0)
+            n1(g + 1, 1)
             bk_pe(g - 1, 0)
             bk_pe(g - 1, 1)
             bk_pe(g - 1, 2)
@@ -405,8 +409,5 @@ def tile_brainquantumlayer_pb_t_kernel(tc, state, weights, J, theta, lam, mask, 
             dm(g + 1, 3)
             v2(g, 0)
             v2(g, 1)
-            if g == NG - 1:
-                v3(g, 0)
-                v3(g, 1)
             sg(g + 1, 2)
             sg(g + 1, 3)

@@ -65,6 +65,9 @@ def tile_brainquantumlayer_pb_t_kernel(tc, state, weights, J, theta, lam, mask, 
         def ok(g):
             return 0 <= g < NG
 
+        def by_scalar(g):
+            return 0 <= g < NG - 1
+
         def load(g, src, dst_t, tg):
             if not ok(g):
                 return
@@ -226,10 +229,8 @@ def tile_brainquantumlayer_pb_t_kernel(tc, state, weights, J, theta, lam, mask, 
             return nzt_t[(g, b // 2)][:].bitcast(BF16).rearrange("p (r e) -> p e r", e=2)[:, b % 2, :]
 
         def n1(g, b):
-            if not ok(g):
-                return
             if b == B_BLOCKS[0]:
-                nT = work3.tile([P, len(B_BLOCKS), GROUP], F32, tag="nT")
+                nT = work2.tile([P, len(B_BLOCKS), GROUP], F32, tag="nT")
                 nT_t[g] = nT
             nc.scalar.activation(
                 out=nT_t[g][:, B_BLOCKS.index(b), :], in_=noise_view(g, b), func=ACT.Copy, scale=t01[:, b : b + 1]
@@ -296,9 +297,12 @@ def tile_brainquantumlayer_pb_t_kernel(tc, state, weights, J, theta, lam, mask, 
         def v2(g, b):
             if not ok(g):
                 return
-            if b in B_BLOCKS:
+            if by_scalar(g) and b in B_BLOCKS:
                 part = nT_t[g][:, B_BLOCKS.index(b), :]
                 nc.vector.tensor_tensor(out=part, in0=sg_t[(g, b)][:], in1=part, op=ALU.add)
+                if b == B_BLOCKS[-1]:
+                    both = cT_t[g][:, B_BLOCKS[0] : B_BLOCKS[-1] + 1, :]
+                    nc.gpsimd.tensor_tensor(out=both, in0=both, in1=nT_t[g][:], op=ALU.add)
             else:
                 nc.vector.tensor_tensor(out=cT_t[g][:, b, :], in0=sg_t[(g, b)][:], in1=cT_t[g][:, b, :], op=ALU.add)
 
@@ -314,21 +318,7 @@ def tile_brainquantumlayer_pb_t_kernel(tc, state, weights, J, theta, lam, mask, 
                 return
             cb = ps_tp.tile([P, 512], F32, tag="tp")
             for b in range(NB):
-                dst = cb[:, P * b : P * b + P]
-                if b in B_BLOCKS:
-                    nc.tensor.matmul(
-                        out=dst, lhsT=cT_t[g][:, b, P * j : P * j + P], rhs=ident[:], is_transpose=True, start=True, stop=False
-                    )
-                    nc.tensor.matmul(
-                        out=dst,
-                        lhsT=nT_t[g][:, B_BLOCKS.index(b), P * j : P * j + P],
-                        rhs=ident[:],
-                        is_transpose=True,
-                        start=False,
-                        stop=True,
-                    )
-                else:
-                    nc.tensor.transpose(dst, cT_t[g][:, b, P * j : P * j + P], ident[:])
+                nc.tensor.transpose(cb[:, P * b : P * b + P], cT_t[g][:, b, P * j : P * j + P], ident[:])
             cb_t[(g, j)] = cb
 
         def bk_out(g, j):
@@ -342,7 +332,10 @@ def tile_brainquantumlayer_pb_t_kernel(tc, state, weights, J, theta, lam, mask, 
                 in_=cb_t[(g, j)][:].rearrange("p (u e q) -> p u q e", u=2, e=2),
                 func=ACT.Tanh,
             )
-            store(g, j, j + 1)
+            if g == NG - 1:
+                store(g, j, j + 1)
+            elif j == TPG - 1:
+                store(g, 0, TPG)
 
         trs_pe(0, 0)
         trs_pe(0, 1)
@@ -392,22 +385,28 @@ def tile_brainquantumlayer_pb_t_kernel(tc, state, weights, J, theta, lam, mask, 
             trs_out(g + 2, 1, False)
             v3(g, 2)
             v3(g, 3)
-            trn(g + 1, 0)
-            n1(g + 1, 0)
-            n1(g + 1, 1)
+            if by_scalar(g + 1):
+                trn(g + 1, 0)
+                n1(g + 1, 0)
+                n1(g + 1, 1)
+            if g == NG - 1:
+                trn(g, 0)
             bk_pe(g - 1, 0)
             bk_pe(g - 1, 1)
-            bk_pe(g - 1, 2)
             bk_out(g - 1, 0)
             bk_out(g - 1, 1)
-            bk_out(g - 1, 2)
             v1(g, 0)
             v1(g, 1)
-            qt(g + 1)
             qs(g + 1)
+            qt(g + 1)
             dm(g + 1, 2)
             dm(g + 1, 3)
+            bk_pe(g - 1, 2)
+            bk_out(g - 1, 2)
             v2(g, 0)
             v2(g, 1)
+            if g == NG - 1:
+                v3(g, 0)
+                v3(g, 1)
             sg(g + 1, 2)
             sg(g + 1, 3)

@@ -29,7 +29,7 @@ PI_C = 1.509957990978376e-7
 TWO_OVER_PI = 0.6366197723675814
 
 
-B_BLOCKS = (0, 1)
+GP_BLOCKS = (2, 3)
 
 
 def tile_brainquantumlayer_pb_t_kernel(tc, state, weights, J, theta, lam, mask, noise_raw, out):
@@ -53,7 +53,8 @@ def tile_brainquantumlayer_pb_t_kernel(tc, state, weights, J, theta, lam, mask, 
         gs_t = {}
         sT_t = {}
         nzt_t = {}
-        nT_t = {}
+        nw_t = {}
+        wT_t = {}
         cst_t = {}
         css_t = {}
         dm_t = {}
@@ -65,8 +66,8 @@ def tile_brainquantumlayer_pb_t_kernel(tc, state, weights, J, theta, lam, mask, 
         def ok(g):
             return 0 <= g < NG
 
-        def by_scalar(g):
-            return 0 <= g < NG - 1
+        def by_gpsimd(g, b):
+            return b in GP_BLOCKS and g < NG - 1
 
         def load(g, src, dst_t, tg):
             if not ok(g):
@@ -225,16 +226,20 @@ def tile_brainquantumlayer_pb_t_kernel(tc, state, weights, J, theta, lam, mask, 
                 nc.tensor.transpose(nzt[:, P * j : P * j + P], words[:, lo : lo + P], ident[:])
             nzt_t[(g, u)] = nzt
 
-        def noise_view(g, b):
-            return nzt_t[(g, b // 2)][:].bitcast(BF16).rearrange("p (r e) -> p e r", e=2)[:, b % 2, :]
+        def trn_out(g, u, on_scalar):
+            if not ok(g):
+                return
+            if g not in nw_t:
+                nw = work2.tile([P, WIDE], BF16, tag="nw")
+                nw_t[g] = nw
+            words = nw_t[g][:].bitcast(F32)[:, GROUP * u : GROUP * u + GROUP]
+            if on_scalar:
+                nc.scalar.copy(out=words, in_=nzt_t[(g, u)][:])
+            else:
+                nc.vector.tensor_copy(out=words, in_=nzt_t[(g, u)][:])
 
-        def n1(g, b):
-            if b == B_BLOCKS[0]:
-                nT = work2.tile([P, len(B_BLOCKS), GROUP], F32, tag="nT")
-                nT_t[g] = nT
-            nc.scalar.activation(
-                out=nT_t[g][:, B_BLOCKS.index(b), :], in_=noise_view(g, b), func=ACT.Copy, scale=t01[:, b : b + 1]
-            )
+        def noise_view(g, b):
+            return nw_t[g][:].rearrange("p (u r e) -> p u e r", u=2, e=2)[:, b // 2, b % 2, :]
 
         def quant(g, src_t, dst_t, tg):
             if not ok(g):
@@ -282,29 +287,28 @@ def tile_brainquantumlayer_pb_t_kernel(tc, state, weights, J, theta, lam, mask, 
                 op1=ALU.mult,
             )
 
-        def v3(g, b):
+        def v2(g, b):
             if not ok(g):
                 return
+            if g not in wT_t:
+                wT = work3.tile([P, NB, GROUP], F32, tag="wT")
+                wT_t[g] = wT
             nc.vector.scalar_tensor_tensor(
-                out=cT_t[g][:, b, :],
+                out=wT_t[g][:, b, :],
                 in0=noise_view(g, b),
                 scalar=t01[:, b : b + 1],
-                in1=cT_t[g][:, b, :],
+                in1=sg_t[(g, b)][:],
                 op0=ALU.mult,
                 op1=ALU.add,
             )
 
-        def v2(g, b):
-            if not ok(g):
+        def gp_add(g):
+            if not ok(g) or not by_gpsimd(g, GP_BLOCKS[0]):
                 return
-            if by_scalar(g) and b in B_BLOCKS:
-                part = nT_t[g][:, B_BLOCKS.index(b), :]
-                nc.vector.tensor_tensor(out=part, in0=sg_t[(g, b)][:], in1=part, op=ALU.add)
-                if b == B_BLOCKS[-1]:
-                    both = cT_t[g][:, B_BLOCKS[0] : B_BLOCKS[-1] + 1, :]
-                    nc.gpsimd.tensor_tensor(out=both, in0=both, in1=nT_t[g][:], op=ALU.add)
-            else:
-                nc.vector.tensor_tensor(out=cT_t[g][:, b, :], in0=sg_t[(g, b)][:], in1=cT_t[g][:, b, :], op=ALU.add)
+            blocks = slice(GP_BLOCKS[0], GP_BLOCKS[-1] + 1)
+            nc.gpsimd.tensor_tensor(
+                out=cT_t[g][:, blocks, :], in0=cT_t[g][:, blocks, :], in1=wT_t[g][:, blocks, :], op=ALU.add
+            )
 
         def store(g, j_lo, j_hi):
             rows = slice(g * GROUP, (g + 1) * GROUP)
@@ -318,7 +322,16 @@ def tile_brainquantumlayer_pb_t_kernel(tc, state, weights, J, theta, lam, mask, 
                 return
             cb = ps_tp.tile([P, 512], F32, tag="tp")
             for b in range(NB):
-                nc.tensor.transpose(cb[:, P * b : P * b + P], cT_t[g][:, b, P * j : P * j + P], ident[:])
+                terms = [cT_t[g]] if by_gpsimd(g, b) else [cT_t[g], wT_t[g]]
+                for i, term in enumerate(terms):
+                    nc.tensor.matmul(
+                        out=cb[:, P * b : P * b + P],
+                        lhsT=term[:, b, P * j : P * j + P],
+                        rhs=ident[:],
+                        is_transpose=True,
+                        start=i == 0,
+                        stop=i == len(terms) - 1,
+                    )
             cb_t[(g, j)] = cb
 
         def bk_out(g, j):
@@ -354,8 +367,9 @@ def tile_brainquantumlayer_pb_t_kernel(tc, state, weights, J, theta, lam, mask, 
         qs(0)
         qt(0)
         trn(0, 0)
-        n1(0, 0)
-        n1(0, 1)
+        trn_out(0, 0, True)
+        trn(0, 1)
+        trn_out(0, 1, False)
         trs_pe(1, 0)
         trs_out(1, 0, False)
         trs_pe(1, 1)
@@ -368,29 +382,25 @@ def tile_brainquantumlayer_pb_t_kernel(tc, state, weights, J, theta, lam, mask, 
         for g in range(NG + 2):
             v1(g, 2)
             v1(g, 3)
-            trn(g, 1)
             lds(g + 3)
             ldn(g + 3)
             trs_pe(g + 2, 0)
             bk_pe(g - 2, 3)
-            trs_pe(g + 2, 1)
+            trn(g + 1, 0)
             trs_out(g + 2, 0, False)
             bk_out(g - 2, 3)
             v2(g, 2)
             v2(g, 3)
+            gp_add(g)
             dm(g, 0)
             dm(g, 1)
             sg(g, 0)
             sg(g, 1)
+            trs_pe(g + 2, 1)
+            trn_out(g + 1, 0, True)
             trs_out(g + 2, 1, False)
-            v3(g, 2)
-            v3(g, 3)
-            if by_scalar(g + 1):
-                trn(g + 1, 0)
-                n1(g + 1, 0)
-                n1(g + 1, 1)
-            if g == NG - 1:
-                trn(g, 0)
+            trn(g + 1, 1)
+            trn_out(g + 1, 1, False)
             bk_pe(g - 1, 0)
             bk_pe(g - 1, 1)
             bk_out(g - 1, 0)
@@ -399,14 +409,11 @@ def tile_brainquantumlayer_pb_t_kernel(tc, state, weights, J, theta, lam, mask, 
             v1(g, 1)
             qs(g + 1)
             qt(g + 1)
-            dm(g + 1, 2)
-            dm(g + 1, 3)
-            bk_pe(g - 1, 2)
-            bk_out(g - 1, 2)
             v2(g, 0)
             v2(g, 1)
-            if g == NG - 1:
-                v3(g, 0)
-                v3(g, 1)
+            dm(g + 1, 2)
+            dm(g + 1, 3)
             sg(g + 1, 2)
             sg(g + 1, 3)
+            bk_pe(g - 1, 2)
+            bk_out(g - 1, 2)

@@ -40,8 +40,7 @@ def tile_brainquantumlayer_pb_t_kernel(tc, state, weights, J, theta, lam, mask, 
         packs = ctx.enter_context(tc.tile_pool(name="packs", bufs=2))
         work3 = ctx.enter_context(tc.tile_pool(name="work3", bufs=3))
         work2 = ctx.enter_context(tc.tile_pool(name="work2", bufs=2))
-        ps_tp = ctx.enter_context(tc.psum_pool(name="ps_tp", bufs=3))
-        ps_nz = ctx.enter_context(tc.psum_pool(name="ps_nz", bufs=1))
+        ps_tp = ctx.enter_context(tc.psum_pool(name="ps_tp", bufs=4))
         ps_dm = ctx.enter_context(tc.psum_pool(name="ps_dm", bufs=2))
         ps_sg = ctx.enter_context(tc.psum_pool(name="ps_sg", bufs=2))
         ctx.enter_context(tc.manual_schedule())
@@ -220,7 +219,7 @@ def tile_brainquantumlayer_pb_t_kernel(tc, state, weights, J, theta, lam, mask, 
             if not ok(g):
                 return
             words = nz_t[g][:].bitcast(F32)
-            nzt = ps_nz.tile([P, 512], F32, tag="nzt")
+            nzt = ps_tp.tile([P, 512], F32, tag="tp")
             for j in range(TPG):
                 lo = 256 * j + P * u
                 nc.tensor.transpose(nzt[:, P * j : P * j + P], words[:, lo : lo + P], ident[:])
@@ -379,41 +378,42 @@ def tile_brainquantumlayer_pb_t_kernel(tc, state, weights, J, theta, lam, mask, 
         sg(0, 2)
         sg(0, 3)
 
+        trs_pe(2, 0)
         for g in range(NG + 2):
             v1(g, 2)
             v1(g, 3)
             lds(g + 3)
             ldn(g + 3)
-            trs_pe(g + 2, 0)
             bk_pe(g - 2, 3)
+            bk_pe(g - 1, 0)
             trn(g + 1, 0)
             trs_out(g + 2, 0, False)
             bk_out(g - 2, 3)
+            bk_out(g - 1, 0)
+            trn_out(g + 1, 0, True)
+            dm(g, 0)
+            dm(g, 1)
             v2(g, 2)
             v2(g, 3)
             gp_add(g)
-            dm(g, 0)
-            dm(g, 1)
             sg(g, 0)
             sg(g, 1)
-            trs_pe(g + 2, 1)
-            trn_out(g + 1, 0, True)
-            trs_out(g + 2, 1, False)
-            trn(g + 1, 1)
-            trn_out(g + 1, 1, False)
-            bk_pe(g - 1, 0)
-            bk_pe(g - 1, 1)
-            bk_out(g - 1, 0)
-            bk_out(g - 1, 1)
-            v1(g, 0)
-            v1(g, 1)
             qs(g + 1)
             qt(g + 1)
-            v2(g, 0)
-            v2(g, 1)
+            bk_pe(g - 1, 1)
+            trs_pe(g + 2, 1)
+            trn(g + 1, 1)
+            bk_pe(g - 1, 2)
+            trs_pe(g + 3, 0)
+            bk_out(g - 1, 1)
+            trs_out(g + 2, 1, False)
+            bk_out(g - 1, 2)
+            v1(g, 0)
+            v1(g, 1)
             dm(g + 1, 2)
             dm(g + 1, 3)
+            v2(g, 0)
+            v2(g, 1)
             sg(g + 1, 2)
             sg(g + 1, 3)
-            bk_pe(g - 1, 2)
-            bk_out(g - 1, 2)
+            trn_out(g + 1, 1, False)

@@ -279,9 +279,9 @@ def tile_brainquantumlayer_pb_t_kernel(tc, state, weights, J, theta, lam, mask, 
                 cT_t[g] = cT
             nc.vector.scalar_tensor_tensor(
                 out=cT_t[g][:, b, :],
-                in0=dm_t[(g, b)][:],
+                in0=sT_t[g][:, b, :],
                 scalar=lam_sb[:, 0:1],
-                in1=sT_t[g][:, b, :],
+                in1=dm_t[(g, b)][:],
                 op0=ALU.mult,
                 op1=ALU.mult,
             )

@@ -36,8 +36,9 @@ def tile_brainquantumlayer_pb_t_kernel(tc, state, weights, J, theta, lam, mask, 
     nc = tc.nc
     with ExitStack() as ctx:
         const = ctx.enter_context(tc.tile_pool(name="const", bufs=1))
-        loads = ctx.enter_context(tc.tile_pool(name="loads", bufs=3))
+        loads = ctx.enter_context(tc.tile_pool(name="loads", bufs=4))
         packs = ctx.enter_context(tc.tile_pool(name="packs", bufs=2))
+        work4 = ctx.enter_context(tc.tile_pool(name="work4", bufs=4))
         work3 = ctx.enter_context(tc.tile_pool(name="work3", bufs=3))
         work2 = ctx.enter_context(tc.tile_pool(name="work2", bufs=2))
         ps_tp = ctx.enter_context(tc.psum_pool(name="ps_tp", bufs=4))
@@ -181,7 +182,7 @@ def tile_brainquantumlayer_pb_t_kernel(tc, state, weights, J, theta, lam, mask, 
             if h == 0:
                 gst = packs.tile([P, WIDE], BF16, tag="gst", align_bytes=64)
                 gs = packs.tile([P, WIDE], BF16, tag="gs", align_bytes=64)
-                sT = work3.tile([P, NB, GROUP], F32, tag="sT")
+                sT = work4.tile([P, NB, GROUP], F32, tag="sT")
                 gst_t[g] = gst
                 gs_t[g] = gs
                 sT_t[g] = sT
@@ -375,45 +376,47 @@ def tile_brainquantumlayer_pb_t_kernel(tc, state, weights, J, theta, lam, mask, 
         trs_out(1, 1, False)
         dm(0, 2)
         dm(0, 3)
+        trs_pe(2, 0)
+        trs_out(2, 0, False)
         sg(0, 2)
         sg(0, 3)
+        lds(3)
 
-        trs_pe(2, 0)
         for g in range(NG + 2):
             v1(g, 2)
             v1(g, 3)
-            lds(g + 3)
             ldn(g + 3)
-            bk_pe(g - 2, 3)
-            bk_pe(g - 1, 0)
+            lds(g + 4)
             trn(g + 1, 0)
-            trs_out(g + 2, 0, False)
-            bk_out(g - 2, 3)
-            bk_out(g - 1, 0)
+            bk_pe(g - 2, 3)
             trn_out(g + 1, 0, True)
+            bk_out(g - 2, 3)
             dm(g, 0)
             dm(g, 1)
             v2(g, 2)
             v2(g, 3)
             gp_add(g)
+            trs_pe(g + 2, 1)
+            bk_pe(g - 1, 0)
+            trs_out(g + 2, 1, False)
+            bk_out(g - 1, 0)
             sg(g, 0)
             sg(g, 1)
             qs(g + 1)
             qt(g + 1)
-            bk_pe(g - 1, 1)
-            trs_pe(g + 2, 1)
             trn(g + 1, 1)
-            bk_pe(g - 1, 2)
-            trs_pe(g + 3, 0)
-            bk_out(g - 1, 1)
-            trs_out(g + 2, 1, False)
-            bk_out(g - 1, 2)
+            bk_pe(g - 1, 1)
             v1(g, 0)
             v1(g, 1)
+            trn_out(g + 1, 1, False)
+            bk_out(g - 1, 1)
             dm(g + 1, 2)
             dm(g + 1, 3)
+            trs_pe(g + 3, 0)
+            bk_pe(g - 1, 2)
             v2(g, 0)
             v2(g, 1)
+            trs_out(g + 3, 0, False)
+            bk_out(g - 1, 2)
             sg(g + 1, 2)
             sg(g + 1, 3)
-            trn_out(g + 1, 1, False)

@@ -29,7 +29,7 @@ PI_C = 1.509957990978376e-7
 TWO_OVER_PI = 0.6366197723675814
 
 
-GP_BLOCKS = (2, 3)
+GP_BLOCKS = (3,)
 
 
 def tile_brainquantumlayer_pb_t_kernel(tc, state, weights, J, theta, lam, mask, noise_raw, out):
@@ -49,14 +49,12 @@ def tile_brainquantumlayer_pb_t_kernel(tc, state, weights, J, theta, lam, mask, 
         st_t = {}
         nz_t = {}
         xt_t = {}
-        gst_t = {}
-        gs_t = {}
+        both_t = {}
         sT_t = {}
         nzt_t = {}
         nw_t = {}
         wT_t = {}
-        cst_t = {}
-        css_t = {}
+        q_t = {}
         dm_t = {}
         sg_t = {}
         cT_t = {}
@@ -180,14 +178,12 @@ def tile_brainquantumlayer_pb_t_kernel(tc, state, weights, J, theta, lam, mask, 
             if not ok(g):
                 return
             if h == 0:
-                gst = packs.tile([P, WIDE], BF16, tag="gst", align_bytes=64)
-                gs = packs.tile([P, WIDE], BF16, tag="gs", align_bytes=64)
+                both = packs.tile([P, 2 * WIDE], BF16, tag="both", align_bytes=64)
                 sT = work4.tile([P, NB, GROUP], F32, tag="sT")
-                gst_t[g] = gst
-                gs_t[g] = gs
+                both_t[g] = both
                 sT_t[g] = sT
-            gst = gst_t[g]
-            gs = gs_t[g]
+            gs = both_t[g][:, 0:WIDE]
+            gst = both_t[g][:, WIDE : 2 * WIDE]
             sT = sT_t[g]
             xt = xt_t[(g, h)]
             r_lo = 256 * h
@@ -203,7 +199,7 @@ def tile_brainquantumlayer_pb_t_kernel(tc, state, weights, J, theta, lam, mask, 
                     func=ACT.Tanh,
                 )
             nc.scalar.copy(
-                out=gst[:].bitcast(F32).rearrange("p (r u) -> p r u", u=2)[:, r_lo : r_lo + 256, :],
+                out=gst.bitcast(F32).rearrange("p (r u) -> p r u", u=2)[:, r_lo : r_lo + 256, :],
                 in_=xt[:].rearrange("p (u r) -> p r u", u=2),
             )
             if not round_on_scalar:
@@ -241,32 +237,27 @@ def tile_brainquantumlayer_pb_t_kernel(tc, state, weights, J, theta, lam, mask, 
         def noise_view(g, b):
             return nw_t[g][:].rearrange("p (u r e) -> p u e r", u=2, e=2)[:, b // 2, b % 2, :]
 
-        def quant(g, src_t, dst_t, tg):
+        def quant(g):
             if not ok(g):
                 return
-            codes = packs.tile([P, GROUP], U32, tag="c" + tg, align_bytes=64)
-            scales = packs.tile([P, GROUP], U8, tag="s" + tg, align_bytes=64)
-            nc.vector.quantize_mx(out=codes[:].bitcast(FP8X4), scales=scales[:], in_=src_t[g][:])
-            dst_t[g] = (codes, scales)
+            codes = packs.tile([P, 2 * GROUP], U32, tag="codes", align_bytes=64)
+            scales = packs.tile([P, 2 * GROUP], U8, tag="scales", align_bytes=64)
+            nc.vector.quantize_mx(out=codes[:].bitcast(FP8X4), scales=scales[:], in_=both_t[g][:])
+            q_t[g] = (codes, scales)
 
-        def qs(g):
-            quant(g, gs_t, css_t, "ss")
-
-        def qt(g):
-            quant(g, gst_t, cst_t, "st")
-
-        def mx(g, b, pool, tg, wts, moving_t, dst_t):
+        def mx(g, b, pool, tg, wts, part, dst_t):
             if not ok(g):
                 return
-            codes, scales = moving_t[g]
+            codes, scales = q_t[g]
+            rows = slice(GROUP * part, GROUP * part + GROUP)
             acc = pool.tile([P, GROUP], F32, tag=tg)
             cols = slice(P * b, P * b + P)
             nc.tensor.matmul_mx(
                 out=acc[:],
                 lhsT=wts[0][:, cols].bitcast(FP8X4),
                 lhsT_scale=wts[1][:, cols],
-                rhs=codes[:].bitcast(FP8X4),
-                rhs_scale=scales[:],
+                rhs=codes[:, rows].bitcast(FP8X4),
+                rhs_scale=scales[:, rows],
                 start=True,
                 stop=True,
             )
@@ -359,13 +350,12 @@ def tile_brainquantumlayer_pb_t_kernel(tc, state, weights, J, theta, lam, mask, 
         w_w = prepare(w_raw, "w")
 
         def dm(g, b):
-            mx(g, b, ps_dm, "dm", j_w, css_t, dm_t)
+            mx(g, b, ps_dm, "dm", j_w, 0, dm_t)
 
         def sg(g, b):
-            mx(g, b, ps_sg, "sg", w_w, cst_t, sg_t)
+            mx(g, b, ps_sg, "sg", w_w, 1, sg_t)
 
-        qs(0)
-        qt(0)
+        quant(0)
         trn(0, 0)
         trn_out(0, 0, True)
         trn(0, 1)
@@ -402,8 +392,7 @@ def tile_brainquantumlayer_pb_t_kernel(tc, state, weights, J, theta, lam, mask, 
             bk_out(g - 1, 0)
             sg(g, 0)
             sg(g, 1)
-            qs(g + 1)
-            qt(g + 1)
+            quant(g + 1)
             trn(g + 1, 1)
             bk_pe(g - 1, 1)
             v1(g, 0)

@@ -37,6 +37,7 @@ def tile_brainquantumlayer_pb_t_kernel(tc, state, weights, J, theta, lam, mask, 
     with ExitStack() as ctx:
         const = ctx.enter_context(tc.tile_pool(name="const", bufs=1))
         loads = ctx.enter_context(tc.tile_pool(name="loads", bufs=4))
+        rounded = ctx.enter_context(tc.tile_pool(name="rounded", bufs=1))
         packs = ctx.enter_context(tc.tile_pool(name="packs", bufs=2))
         work4 = ctx.enter_context(tc.tile_pool(name="work4", bufs=4))
         work3 = ctx.enter_context(tc.tile_pool(name="work3", bufs=3))
@@ -49,7 +50,8 @@ def tile_brainquantumlayer_pb_t_kernel(tc, state, weights, J, theta, lam, mask, 
         st_t = {}
         nz_t = {}
         xt_t = {}
-        both_t = {}
+        gs_t = {}
+        gst_t = {}
         sT_t = {}
         nzt_t = {}
         nw_t = {}
@@ -91,14 +93,6 @@ def tile_brainquantumlayer_pb_t_kernel(tc, state, weights, J, theta, lam, mask, 
         ident = const.tile([P, P], F32)
         make_identity(nc, ident[:])
 
-        th_c = const.tile([P, NB], BF16)
-        nc.sync.dma_start(
-            out=th_c[:].rearrange("p (u e) -> p u e", u=2),
-            in_=theta.rearrange("(u q e) -> q u e", u=2, e=2),
-        )
-        lam_bf = const.tile([P, 1], BF16)
-        nc.sync.dma_start(out=lam_bf[:], in_=lam.partition_broadcast(P))
-
         st_first = loads.tile([P, WIDE], BF16, tag="st")
         st_t[0] = st_first
 
@@ -108,20 +102,28 @@ def tile_brainquantumlayer_pb_t_kernel(tc, state, weights, J, theta, lam, mask, 
                 in_=state[0:GROUP, :].rearrange("(p j) k -> p j k", j=TPG)[:, 2 * h : 2 * h + 2, :],
             )
 
+        def load_columns(raw, mat, lo, hi):
+            rows = mat.rearrange("(u q e) c -> u q e c", u=2, e=2)
+            for u in range(2):
+                nc.sync.dma_start(out=raw[:, 2 * u : 2 * u + 2, lo:hi], in_=rows[u][:, :, lo:hi])
+
+        j_raw = const.tile([P, 4, NEUR], BF16)
+        m_raw = const.tile([P, 4, NEUR], BF16)
+        w_raw = const.tile([P, 4, NEUR], BF16)
         first_half(0)
-
-        def load_matrix(mat, nm):
-            raw = const.tile([P, 4, NEUR], BF16, name=nm)
-            nc.sync.dma_start(
-                out=raw[:].rearrange("p (u e) c -> p u e c", u=2),
-                in_=mat.rearrange("(u q e) c -> q u e c", u=2, e=2),
-            )
-            return raw
-
-        j_raw = load_matrix(J, "j_raw")
-        m_raw = load_matrix(mask, "m_raw")
+        load_columns(j_raw, J, 0, 256)
+        load_columns(m_raw, mask, 0, 256)
+        load_columns(j_raw, J, 256, NEUR)
+        load_columns(m_raw, mask, 256, NEUR)
+        th_c = const.tile([P, NB], BF16)
+        nc.sync.dma_start(
+            out=th_c[:].rearrange("p (u e) -> p u e", u=2),
+            in_=theta.rearrange("(u q e) -> q u e", u=2, e=2),
+        )
+        lam_bf = const.tile([P, 1], BF16)
+        nc.sync.dma_start(out=lam_bf[:], in_=lam.partition_broadcast(P))
         first_half(1)
-        w_raw = load_matrix(weights, "w_raw")
+        load_columns(w_raw, weights, 0, NEUR)
         ldn(0)
         lds(1)
         ldn(1)
@@ -129,25 +131,27 @@ def tile_brainquantumlayer_pb_t_kernel(tc, state, weights, J, theta, lam, mask, 
         ldn(2)
 
         lam_sb = const.tile([P, 1], F32)
-        nc.vector.tensor_copy(out=lam_sb[:], in_=lam_bf[:])
         k_int = const.tile([P, NB], I32)
-        nc.vector.tensor_scalar_mul(out=k_int[:], in0=th_c[:], scalar1=TWO_OVER_PI)
         ang = const.tile([P, NB], F32)
-        nc.vector.tensor_scalar_mul(out=ang[:], in0=th_c[:], scalar1=2.0)
         k_f = const.tile([P, NB], F32)
-        nc.vector.tensor_copy(out=k_f[:], in_=k_int[:])
-        for part in (PI_A, PI_B, PI_C):
-            nc.vector.scalar_tensor_tensor(
-                out=ang[:], in0=k_f[:], scalar=-part, in1=ang[:], op0=ALU.mult, op1=ALU.add
-            )
         sin_t = const.tile([P, NB], F32)
         t01 = const.tile([P, NB], F32)
+
+        def angles():
+            nc.vector.tensor_copy(out=lam_sb[:], in_=lam_bf[:])
+            nc.vector.tensor_scalar_mul(out=k_int[:], in0=th_c[:], scalar1=TWO_OVER_PI)
+            nc.vector.tensor_scalar_mul(out=ang[:], in0=th_c[:], scalar1=2.0)
+            nc.vector.tensor_copy(out=k_f[:], in_=k_int[:])
+            for part in (PI_A, PI_B, PI_C):
+                nc.vector.scalar_tensor_tensor(
+                    out=ang[:], in0=k_f[:], scalar=-part, in1=ang[:], op0=ALU.mult, op1=ALU.add
+                )
 
         def sine():
             nc.scalar.activation(out=sin_t[:], in_=ang[:], func=ACT.Sin)
             nc.scalar.activation(out=t01[:], in_=sin_t[:], func=ACT.Abs, scale=0.1)
 
-        def prepare(raw, nm):
+        def masked(raw, nm):
             grouped = const.tile([P, 4 * NEUR], BF16, name=nm + "_g", align_bytes=64)
             for u in range(2):
                 nc.vector.tensor_tensor(
@@ -156,6 +160,9 @@ def tile_brainquantumlayer_pb_t_kernel(tc, state, weights, J, theta, lam, mask, 
                     in1=m_raw[:, :, 256 * u : 256 * u + 256].rearrange("p t (q e) -> p e q t", e=2),
                     op=ALU.mult,
                 )
+            return grouped
+
+        def quant_weights(grouped, nm):
             codes = const.tile([P, NEUR], U32, name=nm + "_c", align_bytes=64)
             scales = const.tile([P, NEUR], U8, name=nm + "_s", align_bytes=64)
             nc.vector.quantize_mx(out=codes[:].bitcast(FP8X4), scales=scales[:], in_=grouped[:])
@@ -174,43 +181,56 @@ def tile_brainquantumlayer_pb_t_kernel(tc, state, weights, J, theta, lam, mask, 
                     )
             xt_t[(g, h)] = xt
 
-        def trs_out(g, h, round_on_scalar):
+        def trs_tanh(g, h):
             if not ok(g):
                 return
             if h == 0:
-                both = packs.tile([P, 2 * WIDE], BF16, tag="both", align_bytes=64)
                 sT = work4.tile([P, NB, GROUP], F32, tag="sT")
-                both_t[g] = both
                 sT_t[g] = sT
-            gs = both_t[g][:, 0:WIDE]
-            gst = both_t[g][:, WIDE : 2 * WIDE]
-            sT = sT_t[g]
-            xt = xt_t[(g, h)]
-            r_lo = 256 * h
             nc.scalar.activation(
-                out=sT[:, :, r_lo : r_lo + 256].rearrange("p (u e) r -> p u e r", u=2),
-                in_=xt[:].bitcast(BF16).rearrange("p (u r e) -> p u e r", u=2, e=2),
+                out=sT_t[g][:, :, 256 * h : 256 * h + 256].rearrange("p (u e) r -> p u e r", u=2),
+                in_=xt_t[(g, h)][:].bitcast(BF16).rearrange("p (u r e) -> p u e r", u=2, e=2),
                 func=ACT.Tanh,
             )
-            if round_on_scalar:
+
+        def trs_round(g, h, on_scalar=False):
+            if not ok(g):
+                return
+            if h == 0:
+                gs = rounded.tile([P, WIDE], BF16, tag="gs", align_bytes=64)
+                gs_t[g] = gs
+            gs = gs_t[g][:, 1024 * h : 1024 * h + 1024]
+            if on_scalar:
                 nc.scalar.activation(
-                    out=gs[:, 4 * r_lo : 4 * r_lo + 1024].rearrange("p (r u e) -> p r u e", u=2, e=2),
-                    in_=xt[:].bitcast(BF16).rearrange("p (u r e) -> p r u e", u=2, e=2),
+                    out=gs.rearrange("p (r u e) -> p r u e", u=2, e=2),
+                    in_=xt_t[(g, h)][:].bitcast(BF16).rearrange("p (u r e) -> p r u e", u=2, e=2),
                     func=ACT.Tanh,
                 )
-            nc.scalar.copy(
-                out=gst.bitcast(F32).rearrange("p (r u) -> p r u", u=2)[:, r_lo : r_lo + 256, :],
-                in_=xt[:].rearrange("p (u r) -> p r u", u=2),
-            )
-            if not round_on_scalar:
+            else:
                 nc.gpsimd.tensor_scalar(
-                    out=gs[:, 4 * r_lo : 4 * r_lo + 1024].rearrange("p (r t) -> p r t", t=4),
-                    in0=sT[:, :, r_lo : r_lo + 256].rearrange("p t r -> p r t"),
+                    out=gs.rearrange("p (r t) -> p r t", t=4),
+                    in0=sT_t[g][:, :, 256 * h : 256 * h + 256].rearrange("p t r -> p r t"),
                     scalar1=1.0,
                     scalar2=0.0,
                     op0=ALU.mult,
                     op1=ALU.add,
                 )
+
+        def trs_copy(g, h):
+            if not ok(g):
+                return
+            if h == 0:
+                gst = packs.tile([P, WIDE], BF16, tag="gst", align_bytes=64)
+                gst_t[g] = gst
+            r_lo = 256 * h
+            nc.scalar.copy(
+                out=gst_t[g][:].bitcast(F32).rearrange("p (r u) -> p r u", u=2)[:, r_lo : r_lo + 256, :],
+                in_=xt_t[(g, h)][:].rearrange("p (u r) -> p r u", u=2),
+            )
+
+        def trs_out(g, h):
+            trs_tanh(g, h)
+            trs_copy(g, h)
 
         def trn(g, u):
             if not ok(g):
@@ -237,27 +257,27 @@ def tile_brainquantumlayer_pb_t_kernel(tc, state, weights, J, theta, lam, mask, 
         def noise_view(g, b):
             return nw_t[g][:].rearrange("p (u r e) -> p u e r", u=2, e=2)[:, b // 2, b % 2, :]
 
-        def quant(g):
+        def quant(g, part):
             if not ok(g):
                 return
-            codes = packs.tile([P, 2 * GROUP], U32, tag="codes", align_bytes=64)
-            scales = packs.tile([P, 2 * GROUP], U8, tag="scales", align_bytes=64)
-            nc.vector.quantize_mx(out=codes[:].bitcast(FP8X4), scales=scales[:], in_=both_t[g][:])
-            q_t[g] = (codes, scales)
+            codes = packs.tile([P, GROUP], U32, tag="codes%d" % part, align_bytes=64)
+            scales = packs.tile([P, GROUP], U8, tag="scales%d" % part, align_bytes=64)
+            source = (gs_t, gst_t)[part][g]
+            nc.vector.quantize_mx(out=codes[:].bitcast(FP8X4), scales=scales[:], in_=source[:])
+            q_t[(g, part)] = (codes, scales)
 
         def mx(g, b, pool, tg, wts, part, dst_t):
             if not ok(g):
                 return
-            codes, scales = q_t[g]
-            rows = slice(GROUP * part, GROUP * part + GROUP)
+            codes, scales = q_t[(g, part)]
             acc = pool.tile([P, GROUP], F32, tag=tg)
             cols = slice(P * b, P * b + P)
             nc.tensor.matmul_mx(
                 out=acc[:],
                 lhsT=wts[0][:, cols].bitcast(FP8X4),
                 lhsT_scale=wts[1][:, cols],
-                rhs=codes[:, rows].bitcast(FP8X4),
-                rhs_scale=scales[:, rows],
+                rhs=codes[:].bitcast(FP8X4),
+                rhs_scale=scales[:],
                 start=True,
                 stop=True,
             )
@@ -329,7 +349,7 @@ def tile_brainquantumlayer_pb_t_kernel(tc, state, weights, J, theta, lam, mask, 
             if not ok(g):
                 return
             if j == 0:
-                o = work2.tile([P, TPG, NEUR], F32, tag="o")
+                o = work4.tile([P, TPG, NEUR], F32, tag="o")
                 o_t[g] = o
             nc.scalar.activation(
                 out=o_t[g][:, j, :].rearrange("p (u q e) -> p u q e", u=2, e=2),
@@ -342,12 +362,20 @@ def tile_brainquantumlayer_pb_t_kernel(tc, state, weights, J, theta, lam, mask, 
                 store(g, 0, TPG)
 
         trs_pe(0, 0)
+        trs_tanh(0, 0)
+        trs_round(0, 0, True)
+        j_g = masked(j_raw, "j")
+        j_w = quant_weights(j_g, "j")
+        angles()
         trs_pe(0, 1)
-        trs_out(0, 0, True)
-        trs_out(0, 1, True)
+        trs_tanh(0, 1)
+        trs_round(0, 1, True)
+        w_g = masked(w_raw, "w")
+        quant(0, 0)
+        trs_copy(0, 0)
+        trs_copy(0, 1)
+        w_w = quant_weights(w_g, "w")
         sine()
-        j_w = prepare(j_raw, "j")
-        w_w = prepare(w_raw, "w")
 
         def dm(g, b):
             mx(g, b, ps_dm, "dm", j_w, 0, dm_t)
@@ -355,57 +383,74 @@ def tile_brainquantumlayer_pb_t_kernel(tc, state, weights, J, theta, lam, mask, 
         def sg(g, b):
             mx(g, b, ps_sg, "sg", w_w, 1, sg_t)
 
-        quant(0)
         trn(0, 0)
         trn_out(0, 0, True)
-        trn(0, 1)
-        trn_out(0, 1, False)
         trs_pe(1, 0)
-        trs_out(1, 0, False)
-        trs_pe(1, 1)
-        trs_out(1, 1, False)
+        trs_out(1, 0)
+        trs_round(1, 0)
         dm(0, 2)
         dm(0, 3)
-        trs_pe(2, 0)
-        trs_out(2, 0, False)
+        quant(0, 1)
+        trn(0, 1)
+        trs_pe(1, 1)
+        trs_out(1, 1)
+        trs_round(1, 1)
+        v1(0, 2)
+        v1(0, 3)
         sg(0, 2)
         sg(0, 3)
+        trn_out(0, 1, False)
+        trs_pe(2, 0)
+        trs_out(2, 0)
         lds(3)
 
-        for g in range(NG + 2):
-            v1(g, 2)
-            v1(g, 3)
+        for g in range(NG + 1):
             ldn(g + 3)
             lds(g + 4)
+            if g < NG:
+                bk_pe(g - 2, 3)
+            bk_pe(g - 1, 0)
             trn(g + 1, 0)
-            bk_pe(g - 2, 3)
+            if g < NG:
+                bk_out(g - 2, 3)
+            bk_out(g - 1, 0)
             trn_out(g + 1, 0, True)
-            bk_out(g - 2, 3)
             dm(g, 0)
             dm(g, 1)
+            if g >= NG - 1:
+                for j in range(1, TPG):
+                    bk_pe(g - 1, j)
+                    bk_out(g - 1, j)
             v2(g, 2)
             v2(g, 3)
-            gp_add(g)
-            trs_pe(g + 2, 1)
-            bk_pe(g - 1, 0)
-            trs_out(g + 2, 1, False)
-            bk_out(g - 1, 0)
             sg(g, 0)
             sg(g, 1)
-            quant(g + 1)
+            quant(g + 1, 1)
+            quant(g + 1, 0)
+            trs_round(g + 2, 0)
+            gp_add(g)
+            if g < NG - 1:
+                bk_pe(g - 1, 1)
+            trs_pe(g + 2, 1)
             trn(g + 1, 1)
-            bk_pe(g - 1, 1)
+            if g < NG - 1:
+                bk_pe(g - 1, 2)
+            trs_pe(g + 3, 0)
+            if g < NG - 1:
+                bk_out(g - 1, 1)
+            trs_out(g + 2, 1)
+            trs_round(g + 2, 1)
+            if g < NG - 1:
+                bk_out(g - 1, 2)
             v1(g, 0)
             v1(g, 1)
-            trn_out(g + 1, 1, False)
-            bk_out(g - 1, 1)
             dm(g + 1, 2)
             dm(g + 1, 3)
-            trs_pe(g + 3, 0)
-            bk_pe(g - 1, 2)
             v2(g, 0)
             v2(g, 1)
-            trs_out(g + 3, 0, False)
-            bk_out(g - 1, 2)
             sg(g + 1, 2)
             sg(g + 1, 3)
+            trn_out(g + 1, 1, False)
+            v1(g + 1, 2)
+            v1(g + 1, 3)
+            trs_out(g + 3, 0)

@@ -29,9 +29,6 @@ PI_C = 1.509957990978376e-7
 TWO_OVER_PI = 0.6366197723675814
 
 
-GP_BLOCKS = (3,)
-
-
 def tile_brainquantumlayer_pb_t_kernel(tc, state, weights, J, theta, lam, mask, noise_raw, out):
     nc = tc.nc
     with ExitStack() as ctx:
@@ -66,8 +63,11 @@ def tile_brainquantumlayer_pb_t_kernel(tc, state, weights, J, theta, lam, mask, 
         def ok(g):
             return 0 <= g < NG
 
+        def gp_blocks(g):
+            return (2, 3) if g >= NG - 2 else (3,)
+
         def by_gpsimd(g, b):
-            return b in GP_BLOCKS and g < NG - 1
+            return b in gp_blocks(g)
 
         def load(g, src, dst_t, tg):
             if not ok(g):
@@ -102,32 +102,31 @@ def tile_brainquantumlayer_pb_t_kernel(tc, state, weights, J, theta, lam, mask, 
                 in_=state[0:GROUP, :].rearrange("(p j) k -> p j k", j=TPG)[:, 2 * h : 2 * h + 2, :],
             )
 
-        def load_columns(raw, mat, lo, hi):
-            rows = mat.rearrange("(u q e) c -> u q e c", u=2, e=2)
-            for u in range(2):
-                nc.sync.dma_start(out=raw[:, 2 * u : 2 * u + 2, lo:hi], in_=rows[u][:, :, lo:hi])
+        def load_matrix(raw, mat):
+            nc.sync.dma_start(
+                out=raw[:].rearrange("p (u e) c -> p u e c", u=2),
+                in_=mat.rearrange("(u q e) c -> q u e c", u=2, e=2),
+            )
 
+        th_c = const.tile([P, NB], BF16)
+        lam_bf = const.tile([P, 1], BF16)
         j_raw = const.tile([P, 4, NEUR], BF16)
         m_raw = const.tile([P, 4, NEUR], BF16)
         w_raw = const.tile([P, 4, NEUR], BF16)
         first_half(0)
-        load_columns(j_raw, J, 0, 256)
-        load_columns(m_raw, mask, 0, 256)
-        load_columns(j_raw, J, 256, NEUR)
-        load_columns(m_raw, mask, 256, NEUR)
-        th_c = const.tile([P, NB], BF16)
         nc.sync.dma_start(
             out=th_c[:].rearrange("p (u e) -> p u e", u=2),
             in_=theta.rearrange("(u q e) -> q u e", u=2, e=2),
         )
-        lam_bf = const.tile([P, 1], BF16)
-        nc.sync.dma_start(out=lam_bf[:], in_=lam.partition_broadcast(P))
+        load_matrix(j_raw, J)
+        load_matrix(m_raw, mask)
         first_half(1)
-        load_columns(w_raw, weights, 0, NEUR)
-        ldn(0)
+        load_matrix(w_raw, weights)
+        nc.sync.dma_start(out=lam_bf[:], in_=lam.partition_broadcast(P))
         lds(1)
-        ldn(1)
+        ldn(0)
         lds(2)
+        ldn(1)
         ldn(2)
 
         lam_sb = const.tile([P, 1], F32)
@@ -138,7 +137,6 @@ def tile_brainquantumlayer_pb_t_kernel(tc, state, weights, J, theta, lam, mask, 
         t01 = const.tile([P, NB], F32)
 
         def angles():
-            nc.vector.tensor_copy(out=lam_sb[:], in_=lam_bf[:])
             nc.vector.tensor_scalar_mul(out=k_int[:], in0=th_c[:], scalar1=TWO_OVER_PI)
             nc.vector.tensor_scalar_mul(out=ang[:], in0=th_c[:], scalar1=2.0)
             nc.vector.tensor_copy(out=k_f[:], in_=k_int[:])
@@ -163,8 +161,8 @@ def tile_brainquantumlayer_pb_t_kernel(tc, state, weights, J, theta, lam, mask, 
             return grouped
 
         def quant_weights(grouped, nm):
-            codes = const.tile([P, NEUR], U32, name=nm + "_c", align_bytes=64)
-            scales = const.tile([P, NEUR], U8, name=nm + "_s", align_bytes=64)
+            codes = const.tile([P, NEUR], U32, name=nm + "_c", align_bytes=256)
+            scales = const.tile([P, NEUR], U8, name=nm + "_s", align_bytes=256)
             nc.vector.quantize_mx(out=codes[:].bitcast(FP8X4), scales=scales[:], in_=grouped[:])
             return codes, scales
 
@@ -260,8 +258,8 @@ def tile_brainquantumlayer_pb_t_kernel(tc, state, weights, J, theta, lam, mask, 
         def quant(g, part):
             if not ok(g):
                 return
-            codes = packs.tile([P, GROUP], U32, tag="codes%d" % part, align_bytes=64)
-            scales = packs.tile([P, GROUP], U8, tag="scales%d" % part, align_bytes=64)
+            codes = packs.tile([P, GROUP], U32, tag="codes%d" % part, align_bytes=256)
+            scales = packs.tile([P, GROUP], U8, tag="scales%d" % part, align_bytes=256)
             source = (gs_t, gst_t)[part][g]
             nc.vector.quantize_mx(out=codes[:].bitcast(FP8X4), scales=scales[:], in_=source[:])
             q_t[(g, part)] = (codes, scales)
@@ -298,25 +296,25 @@ def tile_brainquantumlayer_pb_t_kernel(tc, state, weights, J, theta, lam, mask, 
                 op1=ALU.mult,
             )
 
-        def v2(g, b):
+        def v2(g, b, lo=0, hi=GROUP):
             if not ok(g):
                 return
             if g not in wT_t:
                 wT = work3.tile([P, NB, GROUP], F32, tag="wT")
                 wT_t[g] = wT
             nc.vector.scalar_tensor_tensor(
-                out=wT_t[g][:, b, :],
-                in0=noise_view(g, b),
+                out=wT_t[g][:, b, lo:hi],
+                in0=noise_view(g, b)[:, lo:hi],
                 scalar=t01[:, b : b + 1],
-                in1=sg_t[(g, b)][:],
+                in1=sg_t[(g, b)][:, lo:hi],
                 op0=ALU.mult,
                 op1=ALU.add,
             )
 
         def gp_add(g):
-            if not ok(g) or not by_gpsimd(g, GP_BLOCKS[0]):
+            if not ok(g):
                 return
-            blocks = slice(GP_BLOCKS[0], GP_BLOCKS[-1] + 1)
+            blocks = slice(gp_blocks(g)[0], NB)
             nc.gpsimd.tensor_tensor(
                 out=cT_t[g][:, blocks, :], in0=cT_t[g][:, blocks, :], in1=wT_t[g][:, blocks, :], op=ALU.add
             )
@@ -361,21 +359,23 @@ def tile_brainquantumlayer_pb_t_kernel(tc, state, weights, J, theta, lam, mask, 
             elif j == TPG - 1:
                 store(g, 0, TPG)
 
+        angles()
         trs_pe(0, 0)
         trs_tanh(0, 0)
         trs_round(0, 0, True)
         j_g = masked(j_raw, "j")
         j_w = quant_weights(j_g, "j")
-        angles()
         trs_pe(0, 1)
         trs_tanh(0, 1)
-        trs_round(0, 1, True)
-        w_g = masked(w_raw, "w")
-        quant(0, 0)
+        trs_round(0, 1)
         trs_copy(0, 0)
         trs_copy(0, 1)
-        w_w = quant_weights(w_g, "w")
         sine()
+        w_g = masked(w_raw, "w")
+        nc.vector.tensor_copy(out=lam_sb[:], in_=lam_bf[:])
+        quant(0, 1)
+        quant(0, 0)
+        w_w = quant_weights(w_g, "w")
 
         def dm(g, b):
             mx(g, b, ps_dm, "dm", j_w, 0, dm_t)
@@ -383,25 +383,24 @@ def tile_brainquantumlayer_pb_t_kernel(tc, state, weights, J, theta, lam, mask, 
         def sg(g, b):
             mx(g, b, ps_sg, "sg", w_w, 1, sg_t)
 
-        trn(0, 0)
-        trn_out(0, 0, True)
         trs_pe(1, 0)
         trs_out(1, 0)
         trs_round(1, 0)
-        dm(0, 2)
-        dm(0, 3)
-        quant(0, 1)
-        trn(0, 1)
         trs_pe(1, 1)
         trs_out(1, 1)
         trs_round(1, 1)
-        v1(0, 2)
-        v1(0, 3)
+        trn(0, 1)
+        trn_out(0, 1, True)
+        trs_pe(2, 0)
+        dm(0, 2)
+        dm(0, 3)
         sg(0, 2)
         sg(0, 3)
-        trn_out(0, 1, False)
-        trs_pe(2, 0)
+        v1(0, 2)
+        v1(0, 3)
+        trn(0, 0)
         trs_out(2, 0)
+        trn_out(0, 0, True)
         lds(3)
 
         for g in range(NG + 1):
@@ -440,17 +439,21 @@ def tile_brainquantumlayer_pb_t_kernel(tc, state, weights, J, theta, lam, mask, 
                 bk_out(g - 1, 1)
             trs_out(g + 2, 1)
             trs_round(g + 2, 1)
+            if g % 2 == 0:
+                trn_out(g + 1, 1, True)
             if g < NG - 1:
                 bk_out(g - 1, 2)
             v1(g, 0)
             v1(g, 1)
             dm(g + 1, 2)
             dm(g + 1, 3)
-            v2(g, 0)
-            v2(g, 1)
+            for lo, hi in ((0, GROUP),) if g < NG - 1 else ((0, GROUP // 2), (GROUP // 2, GROUP)):
+                v2(g, 0, lo, hi)
+                v2(g, 1, lo, hi)
             sg(g + 1, 2)
             sg(g + 1, 3)
-            trn_out(g + 1, 1, False)
+            if g % 2 == 1:
+                trn_out(g + 1, 1, False)
             v1(g + 1, 2)
             v1(g + 1, 3)
             trs_out(g + 3, 0)

@@ -191,28 +191,30 @@ def tile_brainquantumlayer_pb_t_kernel(tc, state, weights, J, theta, lam, mask, 
                 func=ACT.Tanh,
             )
 
-        def trs_round(g, h, on_scalar=False):
-            if not ok(g):
-                return
+        def trs_round_scalar(g, h):
             if h == 0:
                 gs = rounded.tile([P, WIDE], BF16, tag="gs", align_bytes=64)
                 gs_t[g] = gs
-            gs = gs_t[g][:, 1024 * h : 1024 * h + 1024]
-            if on_scalar:
-                nc.scalar.activation(
-                    out=gs.rearrange("p (r u e) -> p r u e", u=2, e=2),
-                    in_=xt_t[(g, h)][:].bitcast(BF16).rearrange("p (u r e) -> p r u e", u=2, e=2),
-                    func=ACT.Tanh,
-                )
-            else:
-                nc.gpsimd.tensor_scalar(
-                    out=gs.rearrange("p (r t) -> p r t", t=4),
-                    in0=sT_t[g][:, :, 256 * h : 256 * h + 256].rearrange("p t r -> p r t"),
-                    scalar1=1.0,
-                    scalar2=0.0,
-                    op0=ALU.mult,
-                    op1=ALU.add,
-                )
+            nc.scalar.activation(
+                out=gs_t[g][:, 1024 * h : 1024 * h + 1024].rearrange("p (r u e) -> p r u e", u=2, e=2),
+                in_=xt_t[(g, h)][:].bitcast(BF16).rearrange("p (u r e) -> p r u e", u=2, e=2),
+                func=ACT.Tanh,
+            )
+
+        def trs_round(g, lo, hi):
+            if not ok(g):
+                return
+            if lo == 0:
+                gs = rounded.tile([P, WIDE], BF16, tag="gs", align_bytes=64)
+                gs_t[g] = gs
+            nc.gpsimd.tensor_scalar(
+                out=gs_t[g][:, 4 * lo : 4 * hi].rearrange("p (r t) -> p r t", t=4),
+                in0=sT_t[g][:, :, lo:hi].rearrange("p t r -> p r t"),
+                scalar1=1.0,
+                scalar2=0.0,
+                op0=ALU.mult,
+                op1=ALU.add,
+            )
 
         def trs_copy(g, h):
             if not ok(g):
@@ -362,12 +364,12 @@ def tile_brainquantumlayer_pb_t_kernel(tc, state, weights, J, theta, lam, mask, 
         angles()
         trs_pe(0, 0)
         trs_tanh(0, 0)
-        trs_round(0, 0, True)
+        trs_round_scalar(0, 0)
         j_g = masked(j_raw, "j")
         j_w = quant_weights(j_g, "j")
         trs_pe(0, 1)
         trs_tanh(0, 1)
-        trs_round(0, 1)
+        trs_round_scalar(0, 1)
         trs_copy(0, 0)
         trs_copy(0, 1)
         sine()
@@ -385,10 +387,10 @@ def tile_brainquantumlayer_pb_t_kernel(tc, state, weights, J, theta, lam, mask, 
 
         trs_pe(1, 0)
         trs_out(1, 0)
-        trs_round(1, 0)
+        trs_round(1, 0, GROUP // 2)
         trs_pe(1, 1)
         trs_out(1, 1)
-        trs_round(1, 1)
+        trs_round(1, GROUP // 2, GROUP)
         trn(0, 1)
         trn_out(0, 1, True)
         trs_pe(2, 0)
@@ -409,11 +411,11 @@ def tile_brainquantumlayer_pb_t_kernel(tc, state, weights, J, theta, lam, mask, 
             if g < NG:
                 bk_pe(g - 2, 3)
             bk_pe(g - 1, 0)
-            trn(g + 1, 0)
+            trs_pe(g + 2, 1)
             if g < NG:
                 bk_out(g - 2, 3)
             bk_out(g - 1, 0)
-            trn_out(g + 1, 0, True)
+            trs_out(g + 2, 1)
             dm(g, 0)
             dm(g, 1)
             if g >= NG - 1:
@@ -426,19 +428,18 @@ def tile_brainquantumlayer_pb_t_kernel(tc, state, weights, J, theta, lam, mask, 
             sg(g, 1)
             quant(g + 1, 1)
             quant(g + 1, 0)
-            trs_round(g + 2, 0)
             gp_add(g)
+            trs_round(g + 2, 0, GROUP)
+            trn(g + 1, 0)
+            trn_out(g + 1, 0, True)
             if g < NG - 1:
                 bk_pe(g - 1, 1)
-            trs_pe(g + 2, 1)
             trn(g + 1, 1)
             if g < NG - 1:
                 bk_pe(g - 1, 2)
             trs_pe(g + 3, 0)
             if g < NG - 1:
                 bk_out(g - 1, 1)
-            trs_out(g + 2, 1)
-            trs_round(g + 2, 1)
             if g % 2 == 0:
                 trn_out(g + 1, 1, True)
             if g < NG - 1:

from contextlib import ExitStack

import concourse.mybir as mybir
from concourse.masks import make_identity

F32 = mybir.dt.float32
BF16 = mybir.dt.bfloat16
I32 = mybir.dt.int32
U32 = mybir.dt.uint32
U8 = mybir.dt.uint8
FP8X4 = mybir.dt.float8_e4m3fn_x4
ACT = mybir.ActivationFunctionType
ALU = mybir.AluOpType

P = 128
ROWS = 8192
NEUR = 512
TPG = 4
GROUP = P * TPG
NG = ROWS // GROUP
WIDE = TPG * NEUR
NB = 4

FLOPS = 2 * 2 * ROWS * NEUR * NEUR

PI_A = 3.140625
PI_B = 9.67502593994140625e-4
PI_C = 1.509957990978376e-7
TWO_OVER_PI = 0.6366197723675814


def tile_brainquantumlayer_pb_t_kernel(tc, state, weights, J, theta, lam, mask, noise_raw, out):
    nc = tc.nc
    with ExitStack() as ctx:
        const = ctx.enter_context(tc.tile_pool(name="const", bufs=1))
        loads = ctx.enter_context(tc.tile_pool(name="loads", bufs=4))
        rounded = ctx.enter_context(tc.tile_pool(name="rounded", bufs=1))
        packs = ctx.enter_context(tc.tile_pool(name="packs", bufs=2))
        work4 = ctx.enter_context(tc.tile_pool(name="work4", bufs=4))
        work3 = ctx.enter_context(tc.tile_pool(name="work3", bufs=3))
        work2 = ctx.enter_context(tc.tile_pool(name="work2", bufs=2))
        ps_tp = ctx.enter_context(tc.psum_pool(name="ps_tp", bufs=4))
        ps_dm = ctx.enter_context(tc.psum_pool(name="ps_dm", bufs=2))
        ps_sg = ctx.enter_context(tc.psum_pool(name="ps_sg", bufs=2))
        ctx.enter_context(tc.manual_schedule())

        st_t = {}
        nz_t = {}
        xt_t = {}
        gs_t = {}
        gst_t = {}
        sT_t = {}
        nzt_t = {}
        nw_t = {}
        wT_t = {}
        q_t = {}
        dm_t = {}
        sg_t = {}
        cT_t = {}
        cb_t = {}
        o_t = {}

        def ok(g):
            return 0 <= g < NG

        def gp_blocks(g):
            return (2, 3) if g >= NG - 2 else (3,)

        def by_gpsimd(g, b):
            return b in gp_blocks(g)

        def load(g, src, dst_t, tg):
            if not ok(g):
                return
            rows = slice(g * GROUP, (g + 1) * GROUP)
            t = loads.tile([P, WIDE], BF16, tag=tg)
            nc.sync.dma_start(
                out=t[:].rearrange("p (j k) -> p j k", j=TPG),
                in_=src[rows, :].rearrange("(p j) k -> p j k", j=TPG),
            )
            dst_t[g] = t

        def lds(g):
            load(g, state, st_t, "st")

        def ldn(g):
            load(g, noise_raw, nz_t, "nz")

        seed = const.tile([P, 1], F32)
        nc.vector.memset(seed[:], 0.0)
        seed_out = const.tile([P, 1], F32)
        nc.scalar.activation(out=seed_out[:], in_=seed[:], func=ACT.Silu)
        ident = const.tile([P, P], F32)
        make_identity(nc, ident[:])

        st_first = loads.tile([P, WIDE], BF16, tag="st")
        st_t[0] = st_first

        def first_half(h):
            nc.sync.dma_start(
                out=st_first[:, 1024 * h : 1024 * h + 1024].rearrange("p (j k) -> p j k", j=2),
                in_=state[0:GROUP, :].rearrange("(p j) k -> p j k", j=TPG)[:, 2 * h : 2 * h + 2, :],
            )

        def load_matrix(raw, mat):
            nc.sync.dma_start(
                out=raw[:].rearrange("p (u e) c -> p u e c", u=2),
                in_=mat.rearrange("(u q e) c -> q u e c", u=2, e=2),
            )

        th_c = const.tile([P, NB], BF16)
        lam_bf = const.tile([P, 1], BF16)
        j_raw = const.tile([P, 4, NEUR], BF16)
        m_raw = const.tile([P, 4, NEUR], BF16)
        w_raw = const.tile([P, 4, NEUR], BF16)
        first_half(0)
        nc.sync.dma_start(
            out=th_c[:].rearrange("p (u e) -> p u e", u=2),
            in_=theta.rearrange("(u q e) -> q u e", u=2, e=2),
        )
        load_matrix(j_raw, J)
        load_matrix(m_raw, mask)
        first_half(1)
        load_matrix(w_raw, weights)
        nc.sync.dma_start(out=lam_bf[:], in_=lam.partition_broadcast(P))
        lds(1)
        ldn(0)
        lds(2)
        ldn(1)
        ldn(2)

        lam_sb = const.tile([P, 1], F32)
        k_int = const.tile([P, NB], I32)
        ang = const.tile([P, NB], F32)
        k_f = const.tile([P, NB], F32)
        sin_t = const.tile([P, NB], F32)
        t01 = const.tile([P, NB], F32)

        def angles():
            nc.vector.tensor_scalar_mul(out=k_int[:], in0=th_c[:], scalar1=TWO_OVER_PI)
            nc.vector.tensor_scalar_mul(out=ang[:], in0=th_c[:], scalar1=2.0)
            nc.vector.tensor_copy(out=k_f[:], in_=k_int[:])
            for part in (PI_A, PI_B, PI_C):
                nc.vector.scalar_tensor_tensor(
                    out=ang[:], in0=k_f[:], scalar=-part, in1=ang[:], op0=ALU.mult, op1=ALU.add
                )

        def sine():
            nc.scalar.activation(out=sin_t[:], in_=ang[:], func=ACT.Sin)
            nc.scalar.activation(out=t01[:], in_=sin_t[:], func=ACT.Abs, scale=0.1)

        def masked(raw, nm):
            grouped = const.tile([P, 4 * NEUR], BF16, name=nm + "_g", align_bytes=64)
            for u in range(2):
                nc.vector.tensor_tensor(
                    out=grouped[:, 1024 * u : 1024 * u + 1024].rearrange("p (e q t) -> p e q t", e=2, t=4),
                    in0=raw[:, :, 256 * u : 256 * u + 256].rearrange("p t (q e) -> p e q t", e=2),
                    in1=m_raw[:, :, 256 * u : 256 * u + 256].rearrange("p t (q e) -> p e q t", e=2),
                    op=ALU.mult,
                )
            return grouped

        def quant_weights(grouped, nm):
            codes = const.tile([P, NEUR], U32, name=nm + "_c", align_bytes=256)
            scales = const.tile([P, NEUR], U8, name=nm + "_s", align_bytes=256)
            nc.vector.quantize_mx(out=codes[:].bitcast(FP8X4), scales=scales[:], in_=grouped[:])
            return codes, scales

        def trs_pe(g, h):
            if not ok(g):
                return
            words = st_t[g][:].bitcast(F32)
            xt = ps_tp.tile([P, 512], F32, tag="tp")
            for jj in range(2):
                for u in range(2):
                    lo = 256 * (2 * h + jj) + P * u
                    nc.tensor.transpose(
                        xt[:, 256 * u + P * jj : 256 * u + P * jj + P], words[:, lo : lo + P], ident[:]
                    )
            xt_t[(g, h)] = xt

        def trs_tanh(g, h):
            if not ok(g):
                return
            if h == 0:
                sT = work4.tile([P, NB, GROUP], F32, tag="sT")
                sT_t[g] = sT
            nc.scalar.activation(
                out=sT_t[g][:, :, 256 * h : 256 * h + 256].rearrange("p (u e) r -> p u e r", u=2),
                in_=xt_t[(g, h)][:].bitcast(BF16).rearrange("p (u r e) -> p u e r", u=2, e=2),
                func=ACT.Tanh,
            )

        def trs_round_scalar(g, h):
            if h == 0:
                gs = rounded.tile([P, WIDE], BF16, tag="gs", align_bytes=64)
                gs_t[g] = gs
            nc.scalar.activation(
                out=gs_t[g][:, 1024 * h : 1024 * h + 1024].rearrange("p (r u e) -> p r u e", u=2, e=2),
                in_=xt_t[(g, h)][:].bitcast(BF16).rearrange("p (u r e) -> p r u e", u=2, e=2),
                func=ACT.Tanh,
            )

        def trs_round(g, lo, hi):
            if not ok(g):
                return
            if lo == 0:
                gs = rounded.tile([P, WIDE], BF16, tag="gs", align_bytes=64)
                gs_t[g] = gs
            nc.gpsimd.tensor_scalar(
                out=gs_t[g][:, 4 * lo : 4 * hi].rearrange("p (r t) -> p r t", t=4),
                in0=sT_t[g][:, :, lo:hi].rearrange("p t r -> p r t"),
                scalar1=1.0,
                scalar2=0.0,
                op0=ALU.mult,
                op1=ALU.add,
            )

        def trs_copy(g, h):
            if not ok(g):
                return
            if h == 0:
                gst = packs.tile([P, WIDE], BF16, tag="gst", align_bytes=64)
                gst_t[g] = gst
            r_lo = 256 * h
            nc.scalar.copy(
                out=gst_t[g][:].bitcast(F32).rearrange("p (r u) -> p r u", u=2)[:, r_lo : r_lo + 256, :],
                in_=xt_t[(g, h)][:].rearrange("p (u r) -> p r u", u=2),
            )

        def trs_out(g, h):
            trs_tanh(g, h)
            trs_copy(g, h)

        def trn(g, u):
            if not ok(g):
                return
            words = nz_t[g][:].bitcast(F32)
            nzt = ps_tp.tile([P, 512], F32, tag="tp")
            for j in range(TPG):
                lo = 256 * j + P * u
                nc.tensor.transpose(nzt[:, P * j : P * j + P], words[:, lo : lo + P], ident[:])
            nzt_t[(g, u)] = nzt

        def trn_out(g, u, on_scalar):
            if not ok(g):
                return
            if g not in nw_t:
                nw = work2.tile([P, WIDE], BF16, tag="nw")
                nw_t[g] = nw
            words = nw_t[g][:].bitcast(F32)[:, GROUP * u : GROUP * u + GROUP]
            if on_scalar:
                nc.scalar.copy(out=words, in_=nzt_t[(g, u)][:])
            else:
                nc.vector.tensor_copy(out=words, in_=nzt_t[(g, u)][:])

        def noise_view(g, b):
            return nw_t[g][:].rearrange("p (u r e) -> p u e r", u=2, e=2)[:, b // 2, b % 2, :]

        def quant(g, part):
            if not ok(g):
                return
            codes = packs.tile([P, GROUP], U32, tag="codes%d" % part, align_bytes=256)
            scales = packs.tile([P, GROUP], U8, tag="scales%d" % part, align_bytes=256)
            source = (gs_t, gst_t)[part][g]
            nc.vector.quantize_mx(out=codes[:].bitcast(FP8X4), scales=scales[:], in_=source[:])
            q_t[(g, part)] = (codes, scales)

        def mx(g, b, pool, tg, wts, part, dst_t):
            if not ok(g):
                return
            codes, scales = q_t[(g, part)]
            acc = pool.tile([P, GROUP], F32, tag=tg)
            cols = slice(P * b, P * b + P)
            nc.tensor.matmul_mx(
                out=acc[:],
                lhsT=wts[0][:, cols].bitcast(FP8X4),
                lhsT_scale=wts[1][:, cols],
                rhs=codes[:].bitcast(FP8X4),
                rhs_scale=scales[:],
                start=True,
                stop=True,
            )
            dst_t[(g, b)] = acc

        def v1(g, b):
            if not ok(g):
                return
            if g not in cT_t:
                cT = work3.tile([P, NB, GROUP], F32, tag="cT")
                cT_t[g] = cT
            nc.vector.scalar_tensor_tensor(
                out=cT_t[g][:, b, :],
                in0=sT_t[g][:, b, :],
                scalar=lam_sb[:, 0:1],
                in1=dm_t[(g, b)][:],
                op0=ALU.mult,
                op1=ALU.mult,
            )

        def v2(g, b, lo=0, hi=GROUP):
            if not ok(g):
                return
            if g not in wT_t:
                wT = work3.tile([P, NB, GROUP], F32, tag="wT")
                wT_t[g] = wT
            nc.vector.scalar_tensor_tensor(
                out=wT_t[g][:, b, lo:hi],
                in0=noise_view(g, b)[:, lo:hi],
                scalar=t01[:, b : b + 1],
                in1=sg_t[(g, b)][:, lo:hi],
                op0=ALU.mult,
                op1=ALU.add,
            )

        def gp_add(g):
            if not ok(g):
                return
            blocks = slice(gp_blocks(g)[0], NB)
            nc.gpsimd.tensor_tensor(
                out=cT_t[g][:, blocks, :], in0=cT_t[g][:, blocks, :], in1=wT_t[g][:, blocks, :], op=ALU.add
            )

        def store(g, j_lo, j_hi):
            rows = slice(g * GROUP, (g + 1) * GROUP)
            nc.sync.dma_start(
                out=out[rows, :].rearrange("(p j) n -> p j n", j=TPG)[:, j_lo:j_hi, :],
                in_=o_t[g][:, j_lo:j_hi, :],
            )

        def bk_pe(g, j):
            if not ok(g):
                return
            cb = ps_tp.tile([P, 512], F32, tag="tp")
            for b in range(NB):
                terms = [cT_t[g]] if by_gpsimd(g, b) else [cT_t[g], wT_t[g]]
                for i, term in enumerate(terms):
                    nc.tensor.matmul(
                        out=cb[:, P * b : P * b + P],
                        lhsT=term[:, b, P * j : P * j + P],
                        rhs=ident[:],
                        is_transpose=True,
                        start=i == 0,
                        stop=i == len(terms) - 1,
                    )
            cb_t[(g, j)] = cb

        def bk_out(g, j):
            if not ok(g):
                return
            if j == 0:
                o = work4.tile([P, TPG, NEUR], F32, tag="o")
                o_t[g] = o
            nc.scalar.activation(
                out=o_t[g][:, j, :].rearrange("p (u q e) -> p u q e", u=2, e=2),
                in_=cb_t[(g, j)][:].rearrange("p (u e q) -> p u q e", u=2, e=2),
                func=ACT.Tanh,
            )
            if g == NG - 1:
                store(g, j, j + 1)
            elif j == TPG - 1:
                store(g, 0, TPG)

        angles()
        trs_pe(0, 0)
        trs_tanh(0, 0)
        trs_round_scalar(0, 0)
        j_g = masked(j_raw, "j")
        j_w = quant_weights(j_g, "j")
        trs_pe(0, 1)
        trs_tanh(0, 1)
        trs_round_scalar(0, 1)
        trs_copy(0, 0)
        trs_copy(0, 1)
        sine()
        w_g = masked(w_raw, "w")
        nc.vector.tensor_copy(out=lam_sb[:], in_=lam_bf[:])
        quant(0, 1)
        quant(0, 0)
        w_w = quant_weights(w_g, "w")

        def dm(g, b):
            mx(g, b, ps_dm, "dm", j_w, 0, dm_t)

        def sg(g, b):
            mx(g, b, ps_sg, "sg", w_w, 1, sg_t)

        trs_pe(1, 0)
        trs_out(1, 0)
        trs_round(1, 0, GROUP // 2)
        trs_pe(1, 1)
        trs_out(1, 1)
        trs_round(1, GROUP // 2, GROUP)
        trn(0, 1)
        trn_out(0, 1, True)
        trs_pe(2, 0)
        dm(0, 2)
        dm(0, 3)
        sg(0, 2)
        sg(0, 3)
        v1(0, 2)
        v1(0, 3)
        trn(0, 0)
        trs_out(2, 0)
        trn_out(0, 0, True)
        lds(3)

        for g in range(NG + 1):
            ldn(g + 3)
            lds(g + 4)
            if g < NG:
                bk_pe(g - 2, 3)
            bk_pe(g - 1, 0)
            trs_pe(g + 2, 1)
            if g < NG:
                bk_out(g - 2, 3)
            bk_out(g - 1, 0)
            trs_out(g + 2, 1)
            dm(g, 0)
            dm(g, 1)
            if g >= NG - 1:
                for j in range(1, TPG):
                    bk_pe(g - 1, j)
                    bk_out(g - 1, j)
            v2(g, 2)
            v2(g, 3)
            sg(g, 0)
            sg(g, 1)
            quant(g + 1, 1)
            quant(g + 1, 0)
            gp_add(g)
            trs_round(g + 2, 0, GROUP)
            trn(g + 1, 0)
            trn_out(g + 1, 0, True)
            if g < NG - 1:
                bk_pe(g - 1, 1)
            trn(g + 1, 1)
            if g < NG - 1:
                bk_pe(g - 1, 2)
            trs_pe(g + 3, 0)
            if g < NG - 1:
                bk_out(g - 1, 1)
            if g % 2 == 0:
                trn_out(g + 1, 1, True)
            if g < NG - 1:
                bk_out(g - 1, 2)
            v1(g, 0)
            v1(g, 1)
            dm(g + 1, 2)
            dm(g + 1, 3)
            for lo, hi in ((0, GROUP),) if g < NG - 1 else ((0, GROUP // 2), (GROUP // 2, GROUP)):
                v2(g, 0, lo, hi)
                v2(g, 1, lo, hi)
            sg(g + 1, 2)
            sg(g + 1, 3)
            if g % 2 == 1:
                trn_out(g + 1, 1, False)
            v1(g + 1, 2)
            v1(g + 1, 3)
            trs_out(g + 3, 0)
